import numpy as np
import ml_dtypes


def mxq(x, axis, fmt="e4m3"):
    dtype, down = {"e4m3": (ml_dtypes.float8_e4m3fn, 7), "e5m2": (ml_dtypes.float8_e5m2, 14)}[fmt]
    v = np.moveaxis(np.asarray(x, np.float32).astype(ml_dtypes.bfloat16).astype(np.float64), axis, -1)
    blocks = v.reshape(v.shape[:-1] + (-1, 32))
    amax = np.abs(blocks).max(-1, keepdims=True)
    byte = np.maximum(np.where(amax > 0, np.frexp(amax)[1] - 1 + 127, 0) - down, 1)
    scale = np.exp2(byte - 127.0)
    codes = (blocks / scale).astype(np.float32).astype(dtype).astype(np.float64)
    return np.moveaxis((codes * scale).reshape(v.shape), -1, axis)


WIDE = False


def mx_kscale(k):
    if not WIDE:
        return np.ones(k)
    levels = np.array([10, -10, 5, -5, 0])
    a = np.random.permutation(np.resize(levels, k // 512 * 4)).reshape(k // 512, 4)
    idx = np.arange(k)
    return np.exp2(a[idx // 512, idx % 128 // 32])


BF16 = ml_dtypes.bfloat16


def bf(x):
    return np.asarray(x, np.float32).astype(BF16)


def f64(x):
    return np.asarray(x).astype(np.float64)


E2M1 = np.array([0.0, 0.5, 1.0, 1.5, 2.0, 3.0, 4.0, 6.0, -0.0, -0.5, -1.0, -1.5, -2.0, -3.0, -4.0, -6.0])


def pack_weight(w, fmt):
    k, n = w.shape
    w = f64(bf(w)).reshape(k // 32, 32, n)
    amax = np.abs(w).max(1)
    if fmt == "e4m3":
        byte = np.frexp(amax)[1] - 1 + 127 - 7
    else:
        mant, ex = np.frexp(amax / 6.0)
        byte = np.where(mant > 0.5, ex, ex - 1) + 127
    byte = np.clip(np.where(amax > 0, byte, 1), 1, 254)
    scaled = (w * np.exp2(127.0 - byte)[:, None, :]).reshape(k, n).astype(np.float32)
    by_word = np.ascontiguousarray(scaled.reshape(k // 512, 128, 4, n).transpose(0, 1, 3, 2))
    if fmt == "e4m3":
        words = by_word.astype(ml_dtypes.float8_e4m3fn).view(np.uint8)
    else:
        c = by_word.astype(ml_dtypes.float4_e2m1fn).view(np.uint8) & 0xF
        words = c[..., 0::2] | (c[..., 1::2] << 4)
    return np.ascontiguousarray(words), np.ascontiguousarray(byte.astype(np.uint8).reshape(k // 512, 16, n))


def unpack_weight(words, scales, fmt):
    g, p, n, _ = words.shape
    if fmt == "e4m3":
        vals = np.ascontiguousarray(words).view(ml_dtypes.float8_e4m3fn).astype(np.float64)
    else:
        nib = np.empty((g, p, n, 4), np.uint8)
        nib[..., 0::2] = words & 0xF
        nib[..., 1::2] = words >> 4
        vals = E2M1[nib]
    vals = vals * np.repeat(np.exp2(scales.astype(np.float64) - 127.0), 8, axis=1)[..., None]
    return vals.transpose(0, 1, 3, 2).reshape(g * 512, n)


N, K, IN, HID, OUT = 128, 32, 512, 512, 512
NEG_SLOPE = 0.01
FMT = "e4m3"


def leaky_relu(v):
    return np.where(v >= 0, v, NEG_SLOPE * v)


def safediv(a, b):
    return a / np.where(b == 0, np.ones_like(b), b)


def setup_inputs():
    s = mx_kscale(IN)
    u = mx_kscale(IN + HID)
    un, t = u[:IN], u[IN:]
    g = np.concatenate([np.full(IN, 1.0), np.full(HID, 3.0)])
    centre = np.random.standard_normal((N, 1, IN))
    h_node = bf(np.random.standard_normal((N, IN)) * un)
    h_ngbrs = bf((0.7 * centre + 0.7 * np.random.standard_normal((N, K, IN))) * s)
    alpha = bf(np.random.uniform(0.0, 1.0, (N, K, 1)))
    Wq = np.random.standard_normal((HID, IN)) / np.sqrt(IN) * t[:, None] / s[None, :]
    bq = bf((-0.5 + 0.3 * np.random.standard_normal(HID)) * t)
    Ww = np.random.standard_normal((OUT, IN + HID)) * g[None, :] / np.sqrt(IN + HID) / u[None, :]
    bw = bf(-0.8 + 0.3 * np.random.standard_normal(OUT))
    Wq_words, Wq_scales = pack_weight(np.ascontiguousarray(Wq.T), FMT)
    Ww_words, Ww_scales = pack_weight(np.ascontiguousarray(Ww.T), FMT)
    return {"h_node": h_node,
            "h_ngbrs": h_ngbrs,
            "alpha": alpha,
            "Wq_words": Wq_words,
            "Wq_scales": Wq_scales,
            "bq": bq,
            "Ww_words": Ww_words,
            "Ww_scales": Ww_scales,
            "bw": bw}


def reference(h_node, h_ngbrs, alpha, Wq_words, Wq_scales, bq, Ww_words, Ww_scales, bw):
    a = f64(alpha)
    h1 = leaky_relu((mxq(f64(h_ngbrs), 2, "e4m3") @ unpack_weight(Wq_words, Wq_scales, FMT)) + f64(bq))
    h_agg = safediv((a * h1).sum(axis=1), a.sum(axis=1))
    h_concat = np.concatenate([f64(h_node), h_agg], axis=-1)
    h2 = leaky_relu((mxq(h_concat, 1, "e4m3") @ unpack_weight(Ww_words, Ww_scales, FMT)) + f64(bw))
    nrm = np.sqrt((h2 ** 2).sum(axis=-1, keepdims=True))
    return safediv(h2, nrm)

@@ -1,0 +1,246 @@
+from contextlib import ExitStack
+
+import concourse.mybir as mybir
+from concourse.masks import make_identity
+
+F32 = mybir.dt.float32
+BF16 = mybir.dt.bfloat16
+I32 = mybir.dt.int32
+U32 = mybir.dt.uint32
+U8 = mybir.dt.uint8
+FP8X4 = mybir.dt.float8_e4m3fn_x4
+ALU = mybir.AluOpType
+ACT = mybir.ActivationFunctionType
+AXIS = mybir.AxisListType
+
+P = 128
+NODES = 128
+NGBRS = 32
+FEATS = 512
+PACK = 4
+CHUNKS = FEATS // P
+GROUP = 4
+N_GROUPS = NGBRS // GROUP
+LAG = 2
+NEG_SLOPE = 0.01
+
+FLOPS = 2 * NODES * NGBRS * FEATS * FEATS + 2 * NODES * 2 * FEATS * FEATS
+
+
+def tile_pinsageconv_kernel(
+    tc, h_node, h_ngbrs, alpha, Wq_words, Wq_scales, bq, Ww_words, Ww_scales, bw, out
+):
+    nc = tc.nc
+    with ExitStack() as ctx:
+        consts = ctx.enter_context(tc.tile_pool(name="consts", bufs=1))
+        x_pool = ctx.enter_context(tc.tile_pool(name="x", bufs=N_GROUPS))
+        work = ctx.enter_context(tc.tile_pool(name="work", bufs=3))
+        psum_in = ctx.enter_context(tc.psum_pool(name="psum_in", bufs=2))
+        psum_mx = ctx.enter_context(tc.psum_pool(name="psum_mx", bufs=3))
+        psum_back = ctx.enter_context(tc.psum_pool(name="psum_back", bufs=3))
+
+        w_planes = consts.tile([P, 3, FEATS], U8, align_bytes=64)
+        nc.vector.memset(w_planes[:].rearrange("p w n -> p (w n)").bitcast(I32), 0)
+
+        warm = consts.tile([P, 1], F32)
+        nc.vector.memset(warm[:], 1.0)
+        nc.scalar.sqrt(out=warm[:], in_=warm[:])
+
+        ident_f32 = consts.tile([P, P], F32)
+        make_identity(nc, ident_f32[:])
+        ident_bf16 = consts.tile([P, P], BF16)
+        make_identity(nc, ident_bf16[:])
+
+        x_tiles = {}
+
+        def load_neighbours(g):
+            x_tiles[g] = x_pool.tile([P, GROUP, FEATS], BF16, name="x")
+            nc.sync.dma_start(out=x_tiles[g][:], in_=h_ngbrs[:, GROUP * g : GROUP * (g + 1), :])
+
+        wq_words = consts.tile([P, FEATS], U32, align_bytes=64)
+        ww_words = consts.tile([P, 2, FEATS], U32, align_bytes=64)
+
+        load_neighbours(0)
+        for q in range(4):
+            nc.sync.dma_start(
+                out=w_planes[32 * q : 32 * q + 4, 0, :].bitcast(I32),
+                in_=Wq_scales[0, 4 * q : 4 * q + 4, :].bitcast(I32),
+            )
+        nc.sync.dma_start(
+            out=wq_words[:].bitcast(I32),
+            in_=Wq_words[0].rearrange("p n t -> p (n t)").bitcast(I32),
+        )
+        for g in range(1, N_GROUPS):
+            load_neighbours(g)
+        for g in range(2):
+            nc.sync.dma_start(
+                out=ww_words[:, g, :].bitcast(I32),
+                in_=Ww_words[g].rearrange("p n t -> p (n t)").bitcast(I32),
+            )
+            for q in range(4):
+                nc.sync.dma_start(
+                    out=w_planes[32 * q : 32 * q + 4, 1 + g, :].bitcast(I32),
+                    in_=Ww_scales[g, 4 * q : 4 * q + 4, :].bitcast(I32),
+                )
+
+        alpha_bf = consts.tile([P, NGBRS], BF16)
+        nc.scalar.dma_start(out=alpha_bf[:], in_=alpha.rearrange("n k o -> n (k o)"))
+        bq_rows = consts.tile([P, P], BF16)
+        nc.vector.memset(bq_rows[:], 0.0)
+        nc.scalar.dma_start(out=bq_rows[0:CHUNKS, :], in_=bq.rearrange("(c p) -> c p", p=P))
+        concat = consts.tile([P, 2 * FEATS], BF16)
+        nc.scalar.dma_start(out=concat[:, 0:FEATS], in_=h_node[:, :])
+        bw_all = consts.tile([P, FEATS], BF16)
+        nc.scalar.dma_start(out=bw_all[:], in_=bw.partition_broadcast(P))
+
+        alpha_sum = consts.tile([P, 1], F32)
+        nc.vector.tensor_reduce(out=alpha_sum[:], in_=alpha_bf[:], axis=AXIS.X, op=ALU.add)
+        alpha_den = consts.tile([P, 1], F32)
+        nc.vector.scalar_tensor_tensor(
+            out=alpha_den[:], in0=alpha_sum[:], scalar=0.0, in1=alpha_sum[:],
+            op0=ALU.is_equal, op1=ALU.add,
+        )
+        alpha_inv = consts.tile([P, 1], F32)
+        nc.vector.reciprocal(out=alpha_inv[:], in_=alpha_den[:])
+        weight = consts.tile([P, NGBRS], F32)
+        nc.vector.tensor_scalar_mul(out=weight[:], in0=alpha_bf[:], scalar1=alpha_inv[:, 0:1])
+
+        bq_t = psum_in.tile([P, P], BF16, tag="in")
+        nc.tensor.transpose(bq_t[:], bq_rows[:], ident_bf16[:])
+        bq_cols = consts.tile([P, CHUNKS], F32)
+        nc.vector.tensor_copy(out=bq_cols[:], in_=bq_t[:, 0:CHUNKS])
+
+        sums = [consts.tile([P, FEATS], F32, name="sum%d" % i) for i in range(2)]
+        for i in range(2):
+            nc.vector.memset(sums[i][:], 0.0)
+
+        concat_codes = consts.tile([P, 2, NODES], U32, align_bytes=64)
+        concat_scales = consts.tile([P, 2, NODES], U8, align_bytes=64)
+
+        def quantise_concat_half(g):
+            half_t = psum_in.tile([P, PACK, NODES], BF16, tag="in")
+            for t in range(PACK):
+                nc.tensor.transpose(
+                    half_t[:, t, :], concat[:, FEATS * g + t : FEATS * (g + 1) : PACK], ident_bf16[:]
+                )
+            half_grouped = work.tile([P, NODES, PACK], BF16, align_bytes=64)
+            nc.vector.tensor_copy(out=half_grouped[:], in_=half_t[:].rearrange("p t n -> p n t"))
+            nc.vector.quantize_mx(
+                out=concat_codes[:, g, :].bitcast(FP8X4),
+                scales=concat_scales[:, g, :],
+                in_=half_grouped[:].rearrange("p n t -> p (n t)"),
+            )
+
+        quantise_concat_half(0)
+
+        grouped_of = {}
+        biased_of = {}
+        back_of = {}
+
+        def transpose_group(g):
+            grouped = work.tile([P, GROUP, NODES, PACK], BF16, align_bytes=64)
+            for half in range(GROUP // 2):
+                x_t = psum_in.tile([P, 2, 2, NODES], F32, tag="in")
+                for i in range(2):
+                    words = x_tiles[g][:, 2 * half + i, :].bitcast(F32)
+                    for u in range(2):
+                        nc.tensor.transpose(x_t[:, i, u, :], words[:, u::2], ident_f32[:])
+                nc.scalar.copy(
+                    out=grouped[:, 2 * half : 2 * half + 2, :, :].bitcast(F32),
+                    in_=x_t[:].rearrange("p i u n -> p i n u"),
+                )
+            grouped_of[g] = grouped
+
+        def project_group(g):
+            x_codes = work.tile([P, GROUP * NODES], U32, align_bytes=64)
+            x_scales = work.tile([P, GROUP * NODES], U8, align_bytes=64)
+            nc.vector.quantize_mx(
+                out=x_codes[:].bitcast(FP8X4),
+                scales=x_scales[:],
+                in_=grouped_of[g][:].rearrange("p j n t -> p (j n t)"),
+            )
+            biased = work.tile([P, CHUNKS, GROUP * NODES], F32)
+            for c in range(CHUNKS):
+                cols = slice(P * c, P * (c + 1))
+                z = psum_mx.tile([P, GROUP * NODES], F32, tag="mx")
+                nc.tensor.matmul_mx(
+                    out=z[:],
+                    lhsT=wq_words[:, cols].bitcast(FP8X4),
+                    lhsT_scale=w_planes[:, 0, cols],
+                    rhs=x_codes[:].bitcast(FP8X4),
+                    rhs_scale=x_scales[:],
+                    start=True,
+                    stop=True,
+                )
+                nc.scalar.activation(
+                    out=biased[:, c, :], in_=z[:], func=ACT.Identity, bias=bq_cols[:, c : c + 1], scale=1.0
+                )
+            biased_of[g] = biased
+
+        def add_neighbour(j):
+            total = sums[j % 2]
+            nc.vector.scalar_tensor_tensor(
+                out=total[:], in0=back_of[j][:], scalar=weight[:, j : j + 1], in1=total[:],
+                op0=ALU.mult, op1=ALU.add,
+            )
+
+        def aggregate_group(g):
+            h1 = work.tile([P, CHUNKS, GROUP, NODES], F32)
+            flat = biased_of[g][:].rearrange("p c r -> p (c r)")
+            nc.vector.scalar_tensor_tensor(
+                out=h1[:].rearrange("p c j n -> p (c j n)"), in0=flat, scalar=NEG_SLOPE, in1=flat,
+                op0=ALU.mult, op1=ALU.max,
+            )
+            for i in range(GROUP):
+                j = GROUP * g + i
+                back = psum_back.tile([P, FEATS], F32, tag="back")
+                for c in range(CHUNKS):
+                    nc.tensor.transpose(back[:, P * c : P * (c + 1)], h1[:, c, i, :], ident_f32[:])
+                back_of[j] = back
+                if j >= LAG:
+                    add_neighbour(j - LAG)
+
+        for step in range(N_GROUPS + 2):
+            if step < N_GROUPS:
+                transpose_group(step)
+            if 1 <= step <= N_GROUPS:
+                project_group(step - 1)
+            if step >= 2:
+                aggregate_group(step - 2)
+        for j in range(NGBRS - LAG, NGBRS):
+            add_neighbour(j)
+
+        nc.vector.tensor_tensor(out=concat[:, FEATS : 2 * FEATS], in0=sums[0][:], in1=sums[1][:], op=ALU.add)
+        quantise_concat_half(1)
+
+        z2 = psum_mx.tile([P, FEATS], F32, tag="mx")
+        for g in range(2):
+            nc.tensor.matmul_mx(
+                out=z2[:],
+                lhsT=concat_codes[:, g, :].bitcast(FP8X4),
+                lhsT_scale=concat_scales[:, g, :],
+                rhs=ww_words[:, g, :].bitcast(FP8X4),
+                rhs_scale=w_planes[:, 1 + g, :],
+                start=(g == 0),
+                stop=(g == 1),
+            )
+        biased2 = consts.tile([P, FEATS], F32)
+        nc.vector.tensor_tensor(out=biased2[:], in0=z2[:], in1=bw_all[:], op=ALU.add)
+        h2 = consts.tile([P, FEATS], F32)
+        nc.vector.scalar_tensor_tensor(
+            out=h2[:], in0=biased2[:], scalar=NEG_SLOPE, in1=biased2[:], op0=ALU.mult, op1=ALU.max
+        )
+        squares = consts.tile([P, FEATS], F32)
+        sum_sq = consts.tile([P, 1], F32)
+        nc.scalar.activation(out=squares[:], in_=h2[:], func=ACT.Square, accum_out=sum_sq[:])
+        norm = consts.tile([P, 1], F32)
+        nc.scalar.sqrt(out=norm[:], in_=sum_sq[:])
+        norm_den = consts.tile([P, 1], F32)
+        nc.vector.scalar_tensor_tensor(
+            out=norm_den[:], in0=norm[:], scalar=0.0, in1=norm[:], op0=ALU.is_equal, op1=ALU.add
+        )
+        norm_inv = consts.tile([P, 1], F32)
+        nc.vector.reciprocal(out=norm_inv[:], in_=norm_den[:])
+        result = consts.tile([P, FEATS], F32)
+        nc.vector.tensor_scalar_mul(out=result[:], in0=h2[:], scalar1=norm_inv[:, 0:1])
+        nc.sync.dma_start(out=out[:, :], in_=result[:])

@@ -19,7 +19,7 @@ NGBRS = 32
 FEATS = 512
 PACK = 4
 CHUNKS = FEATS // P
-GROUP = 4
+GROUP = 2
 N_GROUPS = NGBRS // GROUP
 LAG = 2
 NEG_SLOPE = 0.01

@@ -32,6 +32,7 @@ def tile_pinsageconv_kernel(
 ):
     nc = tc.nc
     with ExitStack() as ctx:
+        ctx.enter_context(tc.manual_schedule())
         consts = ctx.enter_context(tc.tile_pool(name="consts", bufs=1))
         x_pool = ctx.enter_context(tc.tile_pool(name="x", bufs=N_GROUPS))
         work = ctx.enter_context(tc.tile_pool(name="work", bufs=3))
@@ -41,9 +42,17 @@ def tile_pinsageconv_kernel(
 
         w_planes = consts.tile([P, 3, FEATS], U8, align_bytes=64)
         nc.vector.memset(w_planes[:].rearrange("p w n -> p (w n)").bitcast(I32), 0)
-
+        bq_rows = consts.tile([P, P], BF16)
+        nc.vector.memset(bq_rows[:], 0.0)
         warm = consts.tile([P, 1], F32)
         nc.vector.memset(warm[:], 1.0)
+
+        alpha_bf = consts.tile([P, NGBRS], BF16)
+        nc.scalar.dma_start(out=alpha_bf[:], in_=alpha.rearrange("n k o -> n (k o)"))
+        nc.scalar.dma_start(out=bq_rows[0:CHUNKS, :], in_=bq.rearrange("(c p) -> c p", p=P))
+        concat = consts.tile([P, 2 * FEATS], BF16)
+        nc.scalar.dma_start(out=concat[:, 0:FEATS], in_=h_node[:, :])
+
         nc.scalar.sqrt(out=warm[:], in_=warm[:])
 
         ident_f32 = consts.tile([P, P], F32)
@@ -59,6 +68,7 @@ def tile_pinsageconv_kernel(
 
         wq_words = consts.tile([P, FEATS], U32, align_bytes=64)
         ww_words = consts.tile([P, 2, FEATS], U32, align_bytes=64)
+        bw_all = consts.tile([P, FEATS], BF16)
 
         load_neighbours(0)
         for q in range(4):
@@ -82,16 +92,11 @@ def tile_pinsageconv_kernel(
                     out=w_planes[32 * q : 32 * q + 4, 1 + g, :].bitcast(I32),
                     in_=Ww_scales[g, 4 * q : 4 * q + 4, :].bitcast(I32),
                 )
+        nc.sync.dma_start(out=bw_all[:], in_=bw.partition_broadcast(P))
 
-        alpha_bf = consts.tile([P, NGBRS], BF16)
-        nc.scalar.dma_start(out=alpha_bf[:], in_=alpha.rearrange("n k o -> n (k o)"))
-        bq_rows = consts.tile([P, P], BF16)
-        nc.vector.memset(bq_rows[:], 0.0)
-        nc.scalar.dma_start(out=bq_rows[0:CHUNKS, :], in_=bq.rearrange("(c p) -> c p", p=P))
-        concat = consts.tile([P, 2 * FEATS], BF16)
-        nc.scalar.dma_start(out=concat[:, 0:FEATS], in_=h_node[:, :])
-        bw_all = consts.tile([P, FEATS], BF16)
-        nc.scalar.dma_start(out=bw_all[:], in_=bw.partition_broadcast(P))
+        sums = [consts.tile([P, FEATS], F32, name="sum%d" % i) for i in range(2)]
+        for i in range(2):
+            nc.vector.memset(sums[i][:], 0.0)
 
         alpha_sum = consts.tile([P, 1], F32)
         nc.vector.tensor_reduce(out=alpha_sum[:], in_=alpha_bf[:], axis=AXIS.X, op=ALU.add)
@@ -105,14 +110,12 @@ def tile_pinsageconv_kernel(
         weight = consts.tile([P, NGBRS], F32)
         nc.vector.tensor_scalar_mul(out=weight[:], in0=alpha_bf[:], scalar1=alpha_inv[:, 0:1])
 
-        bq_t = psum_in.tile([P, P], BF16, tag="in")
-        nc.tensor.transpose(bq_t[:], bq_rows[:], ident_bf16[:])
         bq_cols = consts.tile([P, CHUNKS], F32)
-        nc.vector.tensor_copy(out=bq_cols[:], in_=bq_t[:, 0:CHUNKS])
 
-        sums = [consts.tile([P, FEATS], F32, name="sum%d" % i) for i in range(2)]
-        for i in range(2):
-            nc.vector.memset(sums[i][:], 0.0)
+        def spread_bq():
+            bq_t = psum_in.tile([P, P], BF16, tag="in")
+            nc.tensor.transpose(bq_t[:], bq_rows[:], ident_bf16[:])
+            nc.vector.tensor_copy(out=bq_cols[:], in_=bq_t[:, 0:CHUNKS])
 
         concat_codes = consts.tile([P, 2, NODES], U32, align_bytes=64)
         concat_scales = consts.tile([P, 2, NODES], U8, align_bytes=64)
@@ -131,24 +134,18 @@ def tile_pinsageconv_kernel(
                 in_=half_grouped[:].rearrange("p n t -> p (n t)"),
             )
 
-        quantise_concat_half(0)
-
         grouped_of = {}
         biased_of = {}
         back_of = {}
 
         def transpose_group(g):
             grouped = work.tile([P, GROUP, NODES, PACK], BF16, align_bytes=64)
-            for half in range(GROUP // 2):
-                x_t = psum_in.tile([P, 2, 2, NODES], F32, tag="in")
-                for i in range(2):
-                    words = x_tiles[g][:, 2 * half + i, :].bitcast(F32)
-                    for u in range(2):
-                        nc.tensor.transpose(x_t[:, i, u, :], words[:, u::2], ident_f32[:])
-                nc.scalar.copy(
-                    out=grouped[:, 2 * half : 2 * half + 2, :, :].bitcast(F32),
-                    in_=x_t[:].rearrange("p i u n -> p i n u"),
-                )
+            x_t = psum_in.tile([P, GROUP, 2, NODES], F32, tag="in")
+            for i in range(GROUP):
+                words = x_tiles[g][:, i, :].bitcast(F32)
+                for u in range(2):
+                    nc.tensor.transpose(x_t[:, i, u, :], words[:, u::2], ident_f32[:])
+            nc.scalar.copy(out=grouped[:].bitcast(F32), in_=x_t[:].rearrange("p i u n -> p i n u"))
             grouped_of[g] = grouped
 
         def project_group(g):
@@ -200,10 +197,13 @@ def tile_pinsageconv_kernel(
                 if j >= LAG:
                     add_neighbour(j - LAG)
 
-        for step in range(N_GROUPS + 2):
+        transpose_group(0)
+        spread_bq()
+        quantise_concat_half(0)
+        for step in range(1, N_GROUPS + 2):
             if step < N_GROUPS:
                 transpose_group(step)
-            if 1 <= step <= N_GROUPS:
+            if step <= N_GROUPS:
                 project_group(step - 1)
             if step >= 2:
                 aggregate_group(step - 2)

@@ -111,11 +111,15 @@ def tile_pinsageconv_kernel(
         nc.vector.tensor_scalar_mul(out=weight[:], in0=alpha_bf[:], scalar1=alpha_inv[:, 0:1])
 
         bq_cols = consts.tile([P, CHUNKS], F32)
+        bq_leak = consts.tile([P, CHUNKS], F32)
+        bq_gain = consts.tile([P, CHUNKS], F32)
 
         def spread_bq():
             bq_t = psum_in.tile([P, P], BF16, tag="in")
             nc.tensor.transpose(bq_t[:], bq_rows[:], ident_bf16[:])
             nc.vector.tensor_copy(out=bq_cols[:], in_=bq_t[:, 0:CHUNKS])
+            nc.vector.tensor_scalar_mul(out=bq_leak[:], in0=bq_cols[:], scalar1=NEG_SLOPE)
+            nc.vector.tensor_scalar_mul(out=bq_gain[:], in0=bq_cols[:], scalar1=1.0 - NEG_SLOPE)
 
         concat_codes = consts.tile([P, 2, NODES], U32, align_bytes=64)
         concat_scales = consts.tile([P, 2, NODES], U8, align_bytes=64)
@@ -136,6 +140,8 @@ def tile_pinsageconv_kernel(
 
         grouped_of = {}
         biased_of = {}
+        leak_of = {}
+        gain_of = {}
         back_of = {}
 
         def transpose_group(g):
@@ -156,7 +162,9 @@ def tile_pinsageconv_kernel(
                 scales=x_scales[:],
                 in_=grouped_of[g][:].rearrange("p j n t -> p (j n t)"),
             )
-            biased = work.tile([P, CHUNKS, GROUP * NODES], F32)
+            biased = work.tile([P, CHUNKS // 2, GROUP * NODES], F32)
+            leak = work.tile([P, CHUNKS // 2, GROUP * NODES], F32)
+            gain = work.tile([P, CHUNKS // 2, GROUP * NODES], F32)
             for c in range(CHUNKS):
                 cols = slice(P * c, P * (c + 1))
                 z = psum_mx.tile([P, GROUP * NODES], F32, tag="mx")
@@ -169,10 +177,23 @@ def tile_pinsageconv_kernel(
                     start=True,
                     stop=True,
                 )
-                nc.scalar.activation(
-                    out=biased[:, c, :], in_=z[:], func=ACT.Identity, bias=bq_cols[:, c : c + 1], scale=1.0
-                )
+                if c % 2 == 0:
+                    nc.scalar.activation(
+                        out=biased[:, c // 2, :], in_=z[:], func=ACT.Identity,
+                        bias=bq_cols[:, c : c + 1], scale=1.0,
+                    )
+                else:
+                    nc.scalar.activation(
+                        out=leak[:, c // 2, :], in_=z[:], func=ACT.Identity,
+                        bias=bq_leak[:, c : c + 1], scale=NEG_SLOPE,
+                    )
+                    nc.scalar.activation(
+                        out=gain[:, c // 2, :], in_=z[:], func=ACT.Relu,
+                        bias=bq_gain[:, c : c + 1], scale=1.0 - NEG_SLOPE,
+                    )
             biased_of[g] = biased
+            leak_of[g] = leak
+            gain_of[g] = gain
 
         def add_neighbour(j):
             total = sums[j % 2]
@@ -182,17 +203,29 @@ def tile_pinsageconv_kernel(
             )
 
         def aggregate_group(g):
-            h1 = work.tile([P, CHUNKS, GROUP, NODES], F32)
+            h1 = work.tile([P, CHUNKS // 2, GROUP * NODES], F32)
             flat = biased_of[g][:].rearrange("p c r -> p (c r)")
             nc.vector.scalar_tensor_tensor(
-                out=h1[:].rearrange("p c j n -> p (c j n)"), in0=flat, scalar=NEG_SLOPE, in1=flat,
+                out=h1[:].rearrange("p c r -> p (c r)"), in0=flat, scalar=NEG_SLOPE, in1=flat,
                 op0=ALU.mult, op1=ALU.max,
             )
             for i in range(GROUP):
                 j = GROUP * g + i
+                rows = slice(NODES * i, NODES * (i + 1))
                 back = psum_back.tile([P, FEATS], F32, tag="back")
                 for c in range(CHUNKS):
-                    nc.tensor.transpose(back[:, P * c : P * (c + 1)], h1[:, c, i, :], ident_f32[:])
+                    cols = slice(P * c, P * (c + 1))
+                    if c % 2 == 0:
+                        nc.tensor.transpose(back[:, cols], h1[:, c // 2, rows], ident_f32[:])
+                    else:
+                        nc.tensor.matmul(
+                            out=back[:, cols], lhsT=leak_of[g][:, c // 2, rows], rhs=ident_f32[:],
+                            is_transpose=True, start=True, stop=False,
+                        )
+                        nc.tensor.matmul(
+                            out=back[:, cols], lhsT=gain_of[g][:, c // 2, rows], rhs=ident_f32[:],
+                            is_transpose=True, start=False, stop=True,
+                        )
                 back_of[j] = back
                 if j >= LAG:
                     add_neighbour(j - LAG)
@@ -200,13 +233,13 @@ def tile_pinsageconv_kernel(
         transpose_group(0)
         spread_bq()
         quantise_concat_half(0)
-        for step in range(1, N_GROUPS + 2):
+        for step in range(1, N_GROUPS + 3):
             if step < N_GROUPS:
                 transpose_group(step)
+            if step >= 3:
+                aggregate_group(step - 3)
             if step <= N_GROUPS:
                 project_group(step - 1)
-            if step >= 2:
-                aggregate_group(step - 2)
         for j in range(NGBRS - LAG, NGBRS):
             add_neighbour(j)
 

@@ -18,10 +18,11 @@ NODES = 128
 NGBRS = 32
 FEATS = 512
 PACK = 4
-CHUNKS = FEATS // P
-GROUP = 2
-N_GROUPS = NGBRS // GROUP
-LAG = 2
+PAIR = 2
+N_PAIRS = NGBRS // PAIR
+BLOCK = 4
+PAIRS_IN_BLOCK = BLOCK // PAIR
+N_BLOCKS = NGBRS // BLOCK
 NEG_SLOPE = 0.01
 
 FLOPS = 2 * NODES * NGBRS * FEATS * FEATS + 2 * NODES * 2 * FEATS * FEATS
@@ -34,43 +35,48 @@ def tile_pinsageconv_kernel(
     with ExitStack() as ctx:
         ctx.enter_context(tc.manual_schedule())
         consts = ctx.enter_context(tc.tile_pool(name="consts", bufs=1))
-        x_pool = ctx.enter_context(tc.tile_pool(name="x", bufs=N_GROUPS))
-        work = ctx.enter_context(tc.tile_pool(name="work", bufs=3))
-        psum_in = ctx.enter_context(tc.psum_pool(name="psum_in", bufs=2))
-        psum_mx = ctx.enter_context(tc.psum_pool(name="psum_mx", bufs=3))
-        psum_back = ctx.enter_context(tc.psum_pool(name="psum_back", bufs=3))
+        x_pool = ctx.enter_context(tc.tile_pool(name="x", bufs=N_PAIRS))
+        stage = ctx.enter_context(tc.tile_pool(name="stage", bufs=3))
+        mids = ctx.enter_context(tc.tile_pool(name="mids", bufs=8))
+        terms = ctx.enter_context(tc.tile_pool(name="terms", bufs=16))
+        psum_in = ctx.enter_context(tc.psum_pool(name="psum_in", bufs=3))
+        psum_z = ctx.enter_context(tc.psum_pool(name="psum_z", bufs=4))
+        psum_acc = ctx.enter_context(tc.psum_pool(name="psum_acc", bufs=1))
 
         w_planes = consts.tile([P, 3, FEATS], U8, align_bytes=64)
         nc.vector.memset(w_planes[:].rearrange("p w n -> p (w n)").bitcast(I32), 0)
-        bq_rows = consts.tile([P, P], BF16)
-        nc.vector.memset(bq_rows[:], 0.0)
+        bq_row = consts.tile([P, FEATS], BF16)
+        nc.vector.memset(bq_row[:], 0.0)
+        ones_bf16 = consts.tile([P, P], BF16)
+        nc.vector.memset(ones_bf16[:], 1.0)
         warm = consts.tile([P, 1], F32)
         nc.vector.memset(warm[:], 1.0)
 
         alpha_bf = consts.tile([P, NGBRS], BF16)
         nc.scalar.dma_start(out=alpha_bf[:], in_=alpha.rearrange("n k o -> n (k o)"))
-        nc.scalar.dma_start(out=bq_rows[0:CHUNKS, :], in_=bq.rearrange("(c p) -> c p", p=P))
-        concat = consts.tile([P, 2 * FEATS], BF16)
-        nc.scalar.dma_start(out=concat[:, 0:FEATS], in_=h_node[:, :])
+        nc.scalar.dma_start(out=bq_row[0:1, :], in_=bq.rearrange("(o f) -> o f", o=1))
+        bq_cols_bf = consts.tile([P, PACK], BF16)
+        nc.scalar.dma_start(out=bq_cols_bf[:], in_=bq.rearrange("(p t) -> p t", t=PACK))
+        node_bf = consts.tile([P, FEATS], BF16)
+        nc.scalar.dma_start(out=node_bf[:], in_=h_node[:, :])
 
         nc.scalar.sqrt(out=warm[:], in_=warm[:])
 
         ident_f32 = consts.tile([P, P], F32)
         make_identity(nc, ident_f32[:])
-        ident_bf16 = consts.tile([P, P], BF16)
-        make_identity(nc, ident_bf16[:])
 
         x_tiles = {}
 
-        def load_neighbours(g):
-            x_tiles[g] = x_pool.tile([P, GROUP, FEATS], BF16, name="x")
-            nc.sync.dma_start(out=x_tiles[g][:], in_=h_ngbrs[:, GROUP * g : GROUP * (g + 1), :])
+        def load_pair(g):
+            x_tiles[g] = x_pool.tile([P, PAIR, FEATS], BF16, name="x")
+            nc.sync.dma_start(out=x_tiles[g][:], in_=h_ngbrs[:, PAIR * g : PAIR * (g + 1), :])
 
         wq_words = consts.tile([P, FEATS], U32, align_bytes=64)
         ww_words = consts.tile([P, 2, FEATS], U32, align_bytes=64)
         bw_all = consts.tile([P, FEATS], BF16)
 
-        load_neighbours(0)
+        for g in range(PAIRS_IN_BLOCK):
+            load_pair(g)
         for q in range(4):
             nc.sync.dma_start(
                 out=w_planes[32 * q : 32 * q + 4, 0, :].bitcast(I32),
@@ -80,8 +86,8 @@ def tile_pinsageconv_kernel(
             out=wq_words[:].bitcast(I32),
             in_=Wq_words[0].rearrange("p n t -> p (n t)").bitcast(I32),
         )
-        for g in range(1, N_GROUPS):
-            load_neighbours(g)
+        for g in range(PAIRS_IN_BLOCK, N_PAIRS):
+            load_pair(g)
         for g in range(2):
             nc.sync.dma_start(
                 out=ww_words[:, g, :].bitcast(I32),
@@ -94,10 +100,6 @@ def tile_pinsageconv_kernel(
                 )
         nc.sync.dma_start(out=bw_all[:], in_=bw.partition_broadcast(P))
 
-        sums = [consts.tile([P, FEATS], F32, name="sum%d" % i) for i in range(2)]
-        for i in range(2):
-            nc.vector.memset(sums[i][:], 0.0)
-
         alpha_sum = consts.tile([P, 1], F32)
         nc.vector.tensor_reduce(out=alpha_sum[:], in_=alpha_bf[:], axis=AXIS.X, op=ALU.add)
         alpha_den = consts.tile([P, 1], F32)
@@ -109,154 +111,208 @@ def tile_pinsageconv_kernel(
         nc.vector.reciprocal(out=alpha_inv[:], in_=alpha_den[:])
         weight = consts.tile([P, NGBRS], F32)
         nc.vector.tensor_scalar_mul(out=weight[:], in0=alpha_bf[:], scalar1=alpha_inv[:, 0:1])
+        weight_leak = consts.tile([P, NGBRS], F32)
+        nc.vector.tensor_scalar_mul(out=weight_leak[:], in0=weight[:], scalar1=NEG_SLOPE)
 
-        bq_cols = consts.tile([P, CHUNKS], F32)
-        bq_leak = consts.tile([P, CHUNKS], F32)
-        bq_gain = consts.tile([P, CHUNKS], F32)
-
-        def spread_bq():
-            bq_t = psum_in.tile([P, P], BF16, tag="in")
-            nc.tensor.transpose(bq_t[:], bq_rows[:], ident_bf16[:])
-            nc.vector.tensor_copy(out=bq_cols[:], in_=bq_t[:, 0:CHUNKS])
-            nc.vector.tensor_scalar_mul(out=bq_leak[:], in0=bq_cols[:], scalar1=NEG_SLOPE)
-            nc.vector.tensor_scalar_mul(out=bq_gain[:], in0=bq_cols[:], scalar1=1.0 - NEG_SLOPE)
+        bq_all = psum_z.tile([P, FEATS], F32, tag="z")
+        nc.tensor.matmul(out=bq_all[:], lhsT=ones_bf16[:], rhs=bq_row[:], start=True, stop=True)
+        neg_bq = consts.tile([P, PACK, P], F32)
+        nc.vector.tensor_scalar_mul(
+            out=neg_bq[:], in0=bq_all[:].rearrange("p (m t) -> p t m", t=PACK), scalar1=-1.0
+        )
+        knee = consts.tile([P, PACK, P], F32)
+        nc.vector.tensor_scalar_mul(
+            out=knee[:], in0=bq_all[:].rearrange("p (m t) -> p t m", t=PACK), scalar1=NEG_SLOPE - 1.0
+        )
 
         concat_codes = consts.tile([P, 2, NODES], U32, align_bytes=64)
         concat_scales = consts.tile([P, 2, NODES], U8, align_bytes=64)
-
-        def quantise_concat_half(g):
-            half_t = psum_in.tile([P, PACK, NODES], BF16, tag="in")
-            for t in range(PACK):
-                nc.tensor.transpose(
-                    half_t[:, t, :], concat[:, FEATS * g + t : FEATS * (g + 1) : PACK], ident_bf16[:]
-                )
-            half_grouped = work.tile([P, NODES, PACK], BF16, align_bytes=64)
-            nc.vector.tensor_copy(out=half_grouped[:], in_=half_t[:].rearrange("p t n -> p n t"))
-            nc.vector.quantize_mx(
-                out=concat_codes[:, g, :].bitcast(FP8X4),
-                scales=concat_scales[:, g, :],
-                in_=half_grouped[:].rearrange("p n t -> p (n t)"),
-            )
+        acc = psum_acc.tile([P, PACK, NODES], F32)
 
         grouped_of = {}
-        biased_of = {}
-        leak_of = {}
-        gain_of = {}
-        back_of = {}
+        codes_of = {}
+        scales_of = {}
+        z_of = {}
+        mid_of = {}
+        terms_of = {}
 
-        def transpose_group(g):
-            grouped = work.tile([P, GROUP, NODES, PACK], BF16, align_bytes=64)
-            x_t = psum_in.tile([P, GROUP, 2, NODES], F32, tag="in")
-            for i in range(GROUP):
-                words = x_tiles[g][:, i, :].bitcast(F32)
-                for u in range(2):
-                    nc.tensor.transpose(x_t[:, i, u, :], words[:, u::2], ident_f32[:])
-            nc.scalar.copy(out=grouped[:].bitcast(F32), in_=x_t[:].rearrange("p i u n -> p i n u"))
-            grouped_of[g] = grouped
+        def transpose_words(dest, rows):
+            words = rows.bitcast(F32)
+            for u in range(2):
+                nc.tensor.transpose(dest[:, u, :], words[:, u::2], ident_f32[:])
 
-        def project_group(g):
-            x_codes = work.tile([P, GROUP * NODES], U32, align_bytes=64)
-            x_scales = work.tile([P, GROUP * NODES], U8, align_bytes=64)
+        def transpose_block(b):
+            grouped_of[b] = stage.tile([P, BLOCK, NODES, PACK], BF16, align_bytes=64, name="grouped")
+            for q in range(PAIRS_IN_BLOCK):
+                g = PAIRS_IN_BLOCK * b + q
+                x_t = psum_in.tile([P, PAIR, 2, NODES], F32, tag="in")
+                for i in range(PAIR):
+                    transpose_words(x_t[:, i], x_tiles[g][:, i, :])
+                nc.scalar.copy(
+                    out=grouped_of[b][:, PAIR * q : PAIR * (q + 1)].bitcast(F32),
+                    in_=x_t[:].rearrange("p i u n -> p i n u"),
+                )
+
+        def quantise_block(b):
+            codes_of[b] = stage.tile([P, BLOCK * NODES], U32, align_bytes=64, name="codes")
+            scales_of[b] = stage.tile([P, BLOCK * NODES], U8, align_bytes=64, name="scales")
             nc.vector.quantize_mx(
-                out=x_codes[:].bitcast(FP8X4),
-                scales=x_scales[:],
-                in_=grouped_of[g][:].rearrange("p j n t -> p (j n t)"),
+                out=codes_of[b][:].bitcast(FP8X4),
+                scales=scales_of[b][:],
+                in_=grouped_of[b][:].rearrange("p j n t -> p (j n t)"),
             )
-            biased = work.tile([P, CHUNKS // 2, GROUP * NODES], F32)
-            leak = work.tile([P, CHUNKS // 2, GROUP * NODES], F32)
-            gain = work.tile([P, CHUNKS // 2, GROUP * NODES], F32)
-            for c in range(CHUNKS):
-                cols = slice(P * c, P * (c + 1))
-                z = psum_mx.tile([P, GROUP * NODES], F32, tag="mx")
+
+        def project_block(b):
+            for i in range(BLOCK):
+                cols = slice(NODES * i, NODES * (i + 1))
+                z = psum_z.tile([P, FEATS], F32, tag="z")
                 nc.tensor.matmul_mx(
                     out=z[:],
-                    lhsT=wq_words[:, cols].bitcast(FP8X4),
-                    lhsT_scale=w_planes[:, 0, cols],
-                    rhs=x_codes[:].bitcast(FP8X4),
-                    rhs_scale=x_scales[:],
+                    lhsT=codes_of[b][:, cols].bitcast(FP8X4),
+                    lhsT_scale=scales_of[b][:, cols],
+                    rhs=wq_words[:].bitcast(FP8X4),
+                    rhs_scale=w_planes[:, 0, :],
                     start=True,
                     stop=True,
                 )
-                if c % 2 == 0:
-                    nc.scalar.activation(
-                        out=biased[:, c // 2, :], in_=z[:], func=ACT.Identity,
-                        bias=bq_cols[:, c : c + 1], scale=1.0,
-                    )
-                else:
-                    nc.scalar.activation(
-                        out=leak[:, c // 2, :], in_=z[:], func=ACT.Identity,
-                        bias=bq_leak[:, c : c + 1], scale=NEG_SLOPE,
-                    )
-                    nc.scalar.activation(
-                        out=gain[:, c // 2, :], in_=z[:], func=ACT.Relu,
-                        bias=bq_gain[:, c : c + 1], scale=1.0 - NEG_SLOPE,
-                    )
-            biased_of[g] = biased
-            leak_of[g] = leak
-            gain_of[g] = gain
+                z_of[BLOCK * b + i] = z
 
-        def add_neighbour(j):
-            total = sums[j % 2]
-            nc.vector.scalar_tensor_tensor(
-                out=total[:], in0=back_of[j][:], scalar=weight[:, j : j + 1], in1=total[:],
+        def by_word(z):
+            return z[:].rearrange("p (m t) -> p t m", t=PACK)
+
+        def leak_terms(b):
+            for j in range(BLOCK * b + 1, BLOCK * (b + 1), 2):
+                term = terms.tile([P, PACK, P], F32, name="term")
+                nc.scalar.activation(
+                    out=term[:], in_=by_word(z_of[j]), func=ACT.Copy, scale=weight_leak[:, j : j + 1]
+                )
+                terms_of[j] = [term]
+
+        def elementwise_block(b):
+            for j in range(BLOCK * b, BLOCK * (b + 1), 2):
+                bent = mids.tile([P, PACK, P], F32, name="mid")
+                nc.vector.scalar_tensor_tensor(
+                    out=bent[:], in0=by_word(z_of[j]), scalar=NEG_SLOPE, in1=knee[:],
+                    op0=ALU.mult, op1=ALU.add,
+                )
+                clipped = mids.tile([P, PACK, P], F32, name="mid")
+                nc.vector.tensor_tensor(out=clipped[:], in0=by_word(z_of[j + 1]), in1=neg_bq[:], op=ALU.max)
+                nc.vector.tensor_tensor(out=bent[:], in0=by_word(z_of[j]), in1=bent[:], op=ALU.max)
+                gain = terms.tile([P, PACK, P], F32, name="term")
+                nc.gpsimd.tensor_scalar(
+                    out=gain[:], in0=clipped[:], scalar1=weight[:, j + 1 : j + 2], scalar2=1.0 - NEG_SLOPE,
+                    op0=ALU.mult, op1=ALU.mult,
+                )
+                terms_of[j + 1].append(gain)
+                whole = terms.tile([P, PACK, P], F32, name="term")
+                nc.scalar.activation(out=whole[:], in_=bent[:], func=ACT.Copy, scale=weight[:, j : j + 1])
+                terms_of[j] = [whole]
+
+        def add_block(b):
+            for j in range(BLOCK * b, BLOCK * (b + 1)):
+                for k, term in enumerate(terms_of[j]):
+                    for t in range(PACK):
+                        nc.tensor.matmul(
+                            out=acc[:, t, :], lhsT=term[:, t, :], rhs=ident_f32[:], is_transpose=True,
+                            start=(j == 0 and t == 0),
+                            stop=(j == NGBRS - 1 and k == len(terms_of[j]) - 1 and t == PACK - 1),
+                        )
+
+        node_grouped = consts.tile([P, NODES, PACK], BF16, align_bytes=64)
+
+        def transpose_node():
+            node_t = psum_in.tile([P, 2, NODES], F32, tag="in")
+            transpose_words(node_t, node_bf[:])
+            nc.scalar.copy(out=node_grouped[:].bitcast(F32), in_=node_t[:].rearrange("p u n -> p n u"))
+
+        def quantise_node():
+            nc.vector.quantize_mx(
+                out=concat_codes[:, 0, :].bitcast(FP8X4),
+                scales=concat_scales[:, 0, :],
+                in_=node_grouped[:].rearrange("p n t -> p (n t)"),
+            )
+
+        bias_part = consts.tile([P, PACK, NODES], F32)
+
+        weight_sum = consts.tile([P, 1], F32)
+        sum_wide = consts.tile([P, P], F32)
+        bq_cols = consts.tile([P, PACK], F32)
+        sum_t_of = {}
+
+        def widen_weight_sum():
+            nc.vector.tensor_reduce(out=weight_sum[:], in_=weight[:], axis=AXIS.X, op=ALU.add)
+            nc.vector.tensor_scalar(
+                out=sum_wide[:], in0=ident_f32[:], scalar1=0.0, scalar2=weight_sum[:, 0:1],
                 op0=ALU.mult, op1=ALU.add,
             )
+            nc.vector.tensor_copy(out=bq_cols[:], in_=bq_cols_bf[:])
 
-        def aggregate_group(g):
-            h1 = work.tile([P, CHUNKS // 2, GROUP * NODES], F32)
-            flat = biased_of[g][:].rearrange("p c r -> p (c r)")
-            nc.vector.scalar_tensor_tensor(
-                out=h1[:].rearrange("p c r -> p (c r)"), in0=flat, scalar=NEG_SLOPE, in1=flat,
-                op0=ALU.mult, op1=ALU.max,
-            )
-            for i in range(GROUP):
-                j = GROUP * g + i
-                rows = slice(NODES * i, NODES * (i + 1))
-                back = psum_back.tile([P, FEATS], F32, tag="back")
-                for c in range(CHUNKS):
-                    cols = slice(P * c, P * (c + 1))
-                    if c % 2 == 0:
-                        nc.tensor.transpose(back[:, cols], h1[:, c // 2, rows], ident_f32[:])
-                    else:
-                        nc.tensor.matmul(
-                            out=back[:, cols], lhsT=leak_of[g][:, c // 2, rows], rhs=ident_f32[:],
-                            is_transpose=True, start=True, stop=False,
-                        )
-                        nc.tensor.matmul(
-                            out=back[:, cols], lhsT=gain_of[g][:, c // 2, rows], rhs=ident_f32[:],
-                            is_transpose=True, start=False, stop=True,
-                        )
-                back_of[j] = back
-                if j >= LAG:
-                    add_neighbour(j - LAG)
+        def transpose_weight_sum():
+            sum_t_of[0] = psum_in.tile([P, P], F32, tag="in", name="sum_t")
+            nc.tensor.transpose(sum_t_of[0][:], sum_wide[:], ident_f32[:])
 
-        transpose_group(0)
-        spread_bq()
-        quantise_concat_half(0)
-        for step in range(1, N_GROUPS + 3):
-            if step < N_GROUPS:
-                transpose_group(step)
-            if step >= 3:
-                aggregate_group(step - 3)
-            if step <= N_GROUPS:
-                project_group(step - 1)
-        for j in range(NGBRS - LAG, NGBRS):
-            add_neighbour(j)
+        def spread_bias():
+            for t in range(PACK):
+                nc.vector.tensor_scalar_mul(
+                    out=bias_part[:, t, :], in0=sum_t_of[0][:], scalar1=bq_cols[:, t : t + 1]
+                )
 
-        nc.vector.tensor_tensor(out=concat[:, FEATS : 2 * FEATS], in0=sums[0][:], in1=sums[1][:], op=ALU.add)
-        quantise_concat_half(1)
+        transpose_block(0)
+        transpose_block(1)
+        quantise_block(0)
+        z2 = None
+        for step in range(N_BLOCKS + 1):
+            if step + 1 < N_BLOCKS:
+                quantise_block(step + 1)
+            if step < N_BLOCKS:
+                project_block(step)
+                leak_terms(step)
+            if step + 2 < N_BLOCKS:
+                transpose_block(step + 2)
+            if step == 0:
+                transpose_node()
+            if step == 1:
+                transpose_weight_sum()
+            if step < N_BLOCKS:
+                elementwise_block(step)
+            if step == 0:
+                quantise_node()
+                widen_weight_sum()
+            if step == 1:
+                spread_bias()
+            if step == N_BLOCKS:
+                z2 = psum_z.tile([P, FEATS], F32, tag="z")
+                nc.tensor.matmul_mx(
+                    out=z2[:],
+                    lhsT=concat_codes[:, 0, :].bitcast(FP8X4),
+                    lhsT_scale=concat_scales[:, 0, :],
+                    rhs=ww_words[:, 0, :].bitcast(FP8X4),
+                    rhs_scale=w_planes[:, 1, :],
+                    start=True,
+                    stop=False,
+                )
+            if step >= 1:
+                add_block(step - 1)
 
-        z2 = psum_mx.tile([P, FEATS], F32, tag="mx")
-        for g in range(2):
-            nc.tensor.matmul_mx(
-                out=z2[:],
-                lhsT=concat_codes[:, g, :].bitcast(FP8X4),
-                lhsT_scale=concat_scales[:, g, :],
-                rhs=ww_words[:, g, :].bitcast(FP8X4),
-                rhs_scale=w_planes[:, 1 + g, :],
-                start=(g == 0),
-                stop=(g == 1),
-            )
+        agg_grouped = consts.tile([P, NODES, PACK], BF16, align_bytes=64)
+        nc.vector.tensor_tensor(
+            out=agg_grouped[:], in0=acc[:].rearrange("p t n -> p n t"),
+            in1=bias_part[:].rearrange("p t n -> p n t"), op=ALU.add,
+        )
+        nc.vector.quantize_mx(
+            out=concat_codes[:, 1, :].bitcast(FP8X4),
+            scales=concat_scales[:, 1, :],
+            in_=agg_grouped[:].rearrange("p n t -> p (n t)"),
+        )
+        nc.tensor.matmul_mx(
+            out=z2[:],
+            lhsT=concat_codes[:, 1, :].bitcast(FP8X4),
+            lhsT_scale=concat_scales[:, 1, :],
+            rhs=ww_words[:, 1, :].bitcast(FP8X4),
+            rhs_scale=w_planes[:, 2, :],
+            start=False,
+            stop=True,
+        )
         biased2 = consts.tile([P, FEATS], F32)
         nc.vector.tensor_tensor(out=biased2[:], in0=z2[:], in1=bw_all[:], op=ALU.add)
         h2 = consts.tile([P, FEATS], F32)

@@ -24,6 +24,7 @@ BLOCK = 4
 PAIRS_IN_BLOCK = BLOCK // PAIR
 N_BLOCKS = NGBRS // BLOCK
 NEG_SLOPE = 0.01
+ONE_TERM_EVERY = 4
 
 FLOPS = 2 * NODES * NGBRS * FEATS * FEATS + 2 * NODES * 2 * FEATS * FEATS
 
@@ -113,6 +114,8 @@ def tile_pinsageconv_kernel(
         nc.vector.tensor_scalar_mul(out=weight[:], in0=alpha_bf[:], scalar1=alpha_inv[:, 0:1])
         weight_leak = consts.tile([P, NGBRS], F32)
         nc.vector.tensor_scalar_mul(out=weight_leak[:], in0=weight[:], scalar1=NEG_SLOPE)
+        weight_gain = consts.tile([P, NGBRS], F32)
+        nc.vector.tensor_scalar_mul(out=weight_gain[:], in0=weight[:], scalar1=1.0 - NEG_SLOPE)
 
         bq_all = psum_z.tile([P, FEATS], F32, tag="z")
         nc.tensor.matmul(out=bq_all[:], lhsT=ones_bf16[:], rhs=bq_row[:], start=True, stop=True)
@@ -180,33 +183,53 @@ def tile_pinsageconv_kernel(
         def by_word(z):
             return z[:].rearrange("p (m t) -> p t m", t=PACK)
 
+        def one_term(j):
+            return j % ONE_TERM_EVERY == 0
+
         def leak_terms(b):
-            for j in range(BLOCK * b + 1, BLOCK * (b + 1), 2):
-                term = terms.tile([P, PACK, P], F32, name="term")
-                nc.scalar.activation(
-                    out=term[:], in_=by_word(z_of[j]), func=ACT.Copy, scale=weight_leak[:, j : j + 1]
-                )
-                terms_of[j] = [term]
+            for j in range(BLOCK * b, BLOCK * (b + 1)):
+                if not one_term(j):
+                    term = terms.tile([P, PACK, P], F32, name="term")
+                    nc.scalar.activation(
+                        out=term[:], in_=by_word(z_of[j]), func=ACT.Copy, scale=weight_leak[:, j : j + 1]
+                    )
+                    terms_of[j] = [term]
+
+        def finish_one_term(j):
+            bent = mid_of[j]
+            nc.vector.tensor_tensor(out=bent[:], in0=by_word(z_of[j]), in1=bent[:], op=ALU.max)
+            whole = terms.tile([P, PACK, P], F32, name="term")
+            nc.scalar.activation(out=whole[:], in_=bent[:], func=ACT.Copy, scale=weight[:, j : j + 1])
+            terms_of[j] = [whole]
 
         def elementwise_block(b):
-            for j in range(BLOCK * b, BLOCK * (b + 1), 2):
-                bent = mids.tile([P, PACK, P], F32, name="mid")
-                nc.vector.scalar_tensor_tensor(
-                    out=bent[:], in0=by_word(z_of[j]), scalar=NEG_SLOPE, in1=knee[:],
-                    op0=ALU.mult, op1=ALU.add,
-                )
-                clipped = mids.tile([P, PACK, P], F32, name="mid")
-                nc.vector.tensor_tensor(out=clipped[:], in0=by_word(z_of[j + 1]), in1=neg_bq[:], op=ALU.max)
-                nc.vector.tensor_tensor(out=bent[:], in0=by_word(z_of[j]), in1=bent[:], op=ALU.max)
-                gain = terms.tile([P, PACK, P], F32, name="term")
-                nc.gpsimd.tensor_scalar(
-                    out=gain[:], in0=clipped[:], scalar1=weight[:, j + 1 : j + 2], scalar2=1.0 - NEG_SLOPE,
-                    op0=ALU.mult, op1=ALU.mult,
-                )
-                terms_of[j + 1].append(gain)
-                whole = terms.tile([P, PACK, P], F32, name="term")
-                nc.scalar.activation(out=whole[:], in_=bent[:], func=ACT.Copy, scale=weight[:, j : j + 1])
-                terms_of[j] = [whole]
+            waiting = []
+            for j in range(BLOCK * b, BLOCK * (b + 1)):
+                if one_term(j):
+                    mid_of[j] = mids.tile([P, PACK, P], F32, name="mid")
+                    nc.vector.scalar_tensor_tensor(
+                        out=mid_of[j][:], in0=by_word(z_of[j]), scalar=NEG_SLOPE, in1=knee[:],
+                        op0=ALU.mult, op1=ALU.add,
+                    )
+                else:
+                    clipped = mids.tile([P, PACK, P], F32, name="mid")
+                    nc.vector.tensor_tensor(out=clipped[:], in0=by_word(z_of[j]), in1=neg_bq[:], op=ALU.max)
+                    gain = terms.tile([P, PACK, P], F32, name="term")
+                    if j % 2 == 0:
+                        nc.scalar.activation(
+                            out=gain[:], in_=clipped[:], func=ACT.Copy, scale=weight_gain[:, j : j + 1]
+                        )
+                    else:
+                        nc.gpsimd.tensor_scalar(
+                            out=gain[:], in0=clipped[:], scalar1=weight[:, j : j + 1], scalar2=1.0 - NEG_SLOPE,
+                            op0=ALU.mult, op1=ALU.mult,
+                        )
+                    terms_of[j].append(gain)
+                for earlier in waiting:
+                    finish_one_term(earlier)
+                waiting = [j] if one_term(j) else []
+            for earlier in waiting:
+                finish_one_term(earlier)
 
         def add_block(b):
             for j in range(BLOCK * b, BLOCK * (b + 1)):
@@ -267,6 +290,17 @@ def tile_pinsageconv_kernel(
             if step < N_BLOCKS:
                 project_block(step)
                 leak_terms(step)
+            if step == N_BLOCKS - 1:
+                z2 = psum_in.tile([P, FEATS], F32, tag="in")
+                nc.tensor.matmul_mx(
+                    out=z2[:],
+                    lhsT=concat_codes[:, 0, :].bitcast(FP8X4),
+                    lhsT_scale=concat_scales[:, 0, :],
+                    rhs=ww_words[:, 0, :].bitcast(FP8X4),
+                    rhs_scale=w_planes[:, 1, :],
+                    start=True,
+                    stop=False,
+                )
             if step + 2 < N_BLOCKS:
                 transpose_block(step + 2)
             if step == 0:
@@ -280,17 +314,6 @@ def tile_pinsageconv_kernel(
                 widen_weight_sum()
             if step == 1:
                 spread_bias()
-            if step == N_BLOCKS:
-                z2 = psum_z.tile([P, FEATS], F32, tag="z")
-                nc.tensor.matmul_mx(
-                    out=z2[:],
-                    lhsT=concat_codes[:, 0, :].bitcast(FP8X4),
-                    lhsT_scale=concat_scales[:, 0, :],
-                    rhs=ww_words[:, 0, :].bitcast(FP8X4),
-                    rhs_scale=w_planes[:, 1, :],
-                    start=True,
-                    stop=False,
-                )
             if step >= 1:
                 add_block(step - 1)
 
@@ -313,17 +336,21 @@ def tile_pinsageconv_kernel(
             start=False,
             stop=True,
         )
+        halves = [slice(0, FEATS // 2), slice(FEATS // 2, FEATS)]
         biased2 = consts.tile([P, FEATS], F32)
-        nc.vector.tensor_tensor(out=biased2[:], in0=z2[:], in1=bw_all[:], op=ALU.add)
         h2 = consts.tile([P, FEATS], F32)
-        nc.vector.scalar_tensor_tensor(
-            out=h2[:], in0=biased2[:], scalar=NEG_SLOPE, in1=biased2[:], op0=ALU.mult, op1=ALU.max
-        )
         squares = consts.tile([P, FEATS], F32)
-        sum_sq = consts.tile([P, 1], F32)
-        nc.scalar.activation(out=squares[:], in_=h2[:], func=ACT.Square, accum_out=sum_sq[:])
+        sum_sq = [consts.tile([P, 1], F32, name="sum_sq%d" % i) for i in range(2)]
+        for cols in halves:
+            nc.vector.tensor_tensor(out=biased2[:, cols], in0=z2[:, cols], in1=bw_all[:, cols], op=ALU.add)
+        for i, cols in enumerate(halves):
+            nc.vector.scalar_tensor_tensor(
+                out=h2[:, cols], in0=biased2[:, cols], scalar=NEG_SLOPE, in1=biased2[:, cols],
+                op0=ALU.mult, op1=ALU.max,
+            )
+            nc.scalar.activation(out=squares[:, cols], in_=h2[:, cols], func=ACT.Square, accum_out=sum_sq[i][:])
         norm = consts.tile([P, 1], F32)
-        nc.scalar.sqrt(out=norm[:], in_=sum_sq[:])
+        nc.scalar.activation(out=norm[:], in_=sum_sq[0][:], func=ACT.Sqrt, bias=sum_sq[1][:, 0:1], scale=1.0)
         norm_den = consts.tile([P, 1], F32)
         nc.vector.scalar_tensor_tensor(
             out=norm_den[:], in0=norm[:], scalar=0.0, in1=norm[:], op0=ALU.is_equal, op1=ALU.add
@@ -331,5 +358,6 @@ def tile_pinsageconv_kernel(
         norm_inv = consts.tile([P, 1], F32)
         nc.vector.reciprocal(out=norm_inv[:], in_=norm_den[:])
         result = consts.tile([P, FEATS], F32)
-        nc.vector.tensor_scalar_mul(out=result[:], in0=h2[:], scalar1=norm_inv[:, 0:1])
-        nc.sync.dma_start(out=out[:, :], in_=result[:])
+        for cols, queue in zip(halves, [nc.sync, nc.scalar]):
+            nc.vector.tensor_scalar_mul(out=result[:, cols], in0=h2[:, cols], scalar1=norm_inv[:, 0:1])
+            queue.dma_start(out=out[:, cols], in_=result[:, cols])

@@ -24,7 +24,7 @@ BLOCK = 4
 PAIRS_IN_BLOCK = BLOCK // PAIR
 N_BLOCKS = NGBRS // BLOCK
 NEG_SLOPE = 0.01
-ONE_TERM_EVERY = 4
+KINDS = ["one", "vector", "one", "scalar", "one", "scalar", "one", "vector"]
 
 FLOPS = 2 * NODES * NGBRS * FEATS * FEATS + 2 * NODES * 2 * FEATS * FEATS
 
@@ -38,7 +38,7 @@ def tile_pinsageconv_kernel(
         consts = ctx.enter_context(tc.tile_pool(name="consts", bufs=1))
         x_pool = ctx.enter_context(tc.tile_pool(name="x", bufs=N_PAIRS))
         stage = ctx.enter_context(tc.tile_pool(name="stage", bufs=3))
-        mids = ctx.enter_context(tc.tile_pool(name="mids", bufs=8))
+        mids = ctx.enter_context(tc.tile_pool(name="mids", bufs=12))
         terms = ctx.enter_context(tc.tile_pool(name="terms", bufs=16))
         psum_in = ctx.enter_context(tc.psum_pool(name="psum_in", bufs=3))
         psum_z = ctx.enter_context(tc.psum_pool(name="psum_z", bufs=4))
@@ -56,8 +56,6 @@ def tile_pinsageconv_kernel(
         alpha_bf = consts.tile([P, NGBRS], BF16)
         nc.scalar.dma_start(out=alpha_bf[:], in_=alpha.rearrange("n k o -> n (k o)"))
         nc.scalar.dma_start(out=bq_row[0:1, :], in_=bq.rearrange("(o f) -> o f", o=1))
-        bq_cols_bf = consts.tile([P, PACK], BF16)
-        nc.scalar.dma_start(out=bq_cols_bf[:], in_=bq.rearrange("(p t) -> p t", t=PACK))
         node_bf = consts.tile([P, FEATS], BF16)
         nc.scalar.dma_start(out=node_bf[:], in_=h_node[:, :])
 
@@ -112,21 +110,13 @@ def tile_pinsageconv_kernel(
         nc.vector.reciprocal(out=alpha_inv[:], in_=alpha_den[:])
         weight = consts.tile([P, NGBRS], F32)
         nc.vector.tensor_scalar_mul(out=weight[:], in0=alpha_bf[:], scalar1=alpha_inv[:, 0:1])
-        weight_leak = consts.tile([P, NGBRS], F32)
-        nc.vector.tensor_scalar_mul(out=weight_leak[:], in0=weight[:], scalar1=NEG_SLOPE)
-        weight_gain = consts.tile([P, NGBRS], F32)
-        nc.vector.tensor_scalar_mul(out=weight_gain[:], in0=weight[:], scalar1=1.0 - NEG_SLOPE)
+        weight_drop = consts.tile([P, NGBRS], F32)
+        nc.vector.tensor_scalar_mul(out=weight_drop[:], in0=weight[:], scalar1=NEG_SLOPE - 1.0)
 
         bq_all = psum_z.tile([P, FEATS], F32, tag="z")
         nc.tensor.matmul(out=bq_all[:], lhsT=ones_bf16[:], rhs=bq_row[:], start=True, stop=True)
-        neg_bq = consts.tile([P, PACK, P], F32)
-        nc.vector.tensor_scalar_mul(
-            out=neg_bq[:], in0=bq_all[:].rearrange("p (m t) -> p t m", t=PACK), scalar1=-1.0
-        )
-        knee = consts.tile([P, PACK, P], F32)
-        nc.vector.tensor_scalar_mul(
-            out=knee[:], in0=bq_all[:].rearrange("p (m t) -> p t m", t=PACK), scalar1=NEG_SLOPE - 1.0
-        )
+        bq_wide = consts.tile([P, PACK, P], F32)
+        nc.vector.tensor_copy(out=bq_wide[:], in_=bq_all[:].rearrange("p (m t) -> p t m", t=PACK))
 
         concat_codes = consts.tile([P, 2, NODES], U32, align_bytes=64)
         concat_scales = consts.tile([P, 2, NODES], U8, align_bytes=64)
@@ -183,53 +173,48 @@ def tile_pinsageconv_kernel(
         def by_word(z):
             return z[:].rearrange("p (m t) -> p t m", t=PACK)
 
-        def one_term(j):
-            return j % ONE_TERM_EVERY == 0
+        def weighted(source, j):
+            term = terms.tile([P, PACK, P], F32, name="term")
+            nc.scalar.activation(out=term[:], in_=source[:], func=ACT.Copy, scale=weight[:, j : j + 1])
+            terms_of[j].append(term)
 
-        def leak_terms(b):
-            for j in range(BLOCK * b, BLOCK * (b + 1)):
-                if not one_term(j):
-                    term = terms.tile([P, PACK, P], F32, name="term")
-                    nc.scalar.activation(
-                        out=term[:], in_=by_word(z_of[j]), func=ACT.Copy, scale=weight_leak[:, j : j + 1]
-                    )
-                    terms_of[j] = [term]
+        def add_bias(j):
+            mid_of[j] = mids.tile([P, PACK, P], F32, name="mid")
+            nc.vector.tensor_tensor(out=mid_of[j][:], in0=by_word(z_of[j]), in1=bq_wide[:], op=ALU.add)
+            terms_of[j] = []
+            if KINDS[j % 8] != "one":
+                weighted(mid_of[j], j)
 
-        def finish_one_term(j):
-            bent = mid_of[j]
-            nc.vector.tensor_tensor(out=bent[:], in0=by_word(z_of[j]), in1=bent[:], op=ALU.max)
-            whole = terms.tile([P, PACK, P], F32, name="term")
-            nc.scalar.activation(out=whole[:], in_=bent[:], func=ACT.Copy, scale=weight[:, j : j + 1])
-            terms_of[j] = [whole]
+        def finish(j):
+            u = mid_of[j]
+            if KINDS[j % 8] == "one":
+                nc.vector.scalar_tensor_tensor(
+                    out=u[:], in0=u[:], scalar=NEG_SLOPE, in1=u[:], op0=ALU.mult, op1=ALU.max
+                )
+                weighted(u, j)
+            elif KINDS[j % 8] == "vector":
+                term = terms.tile([P, PACK, P], F32, name="term")
+                nc.vector.tensor_scalar(
+                    out=term[:], in0=u[:], scalar1=0.0, scalar2=weight_drop[:, j : j + 1],
+                    op0=ALU.min, op1=ALU.mult,
+                )
+                terms_of[j].append(term)
+            else:
+                below = mids.tile([P, PACK, P], F32, name="mid")
+                nc.scalar.activation(out=below[:], in_=u[:], func=ACT.Relu, scale=-1.0)
+                term = terms.tile([P, PACK, P], F32, name="term")
+                nc.gpsimd.tensor_scalar(
+                    out=term[:], in0=below[:], scalar1=weight[:, j : j + 1], scalar2=1.0 - NEG_SLOPE,
+                    op0=ALU.mult, op1=ALU.mult,
+                )
+                terms_of[j].append(term)
 
         def elementwise_block(b):
-            waiting = []
-            for j in range(BLOCK * b, BLOCK * (b + 1)):
-                if one_term(j):
-                    mid_of[j] = mids.tile([P, PACK, P], F32, name="mid")
-                    nc.vector.scalar_tensor_tensor(
-                        out=mid_of[j][:], in0=by_word(z_of[j]), scalar=NEG_SLOPE, in1=knee[:],
-                        op0=ALU.mult, op1=ALU.add,
-                    )
-                else:
-                    clipped = mids.tile([P, PACK, P], F32, name="mid")
-                    nc.vector.tensor_tensor(out=clipped[:], in0=by_word(z_of[j]), in1=neg_bq[:], op=ALU.max)
-                    gain = terms.tile([P, PACK, P], F32, name="term")
-                    if j % 2 == 0:
-                        nc.scalar.activation(
-                            out=gain[:], in_=clipped[:], func=ACT.Copy, scale=weight_gain[:, j : j + 1]
-                        )
-                    else:
-                        nc.gpsimd.tensor_scalar(
-                            out=gain[:], in0=clipped[:], scalar1=weight[:, j : j + 1], scalar2=1.0 - NEG_SLOPE,
-                            op0=ALU.mult, op1=ALU.mult,
-                        )
-                    terms_of[j].append(gain)
-                for earlier in waiting:
-                    finish_one_term(earlier)
-                waiting = [j] if one_term(j) else []
-            for earlier in waiting:
-                finish_one_term(earlier)
+            for j in range(BLOCK * b, BLOCK * (b + 1) + 1):
+                if j < BLOCK * (b + 1):
+                    add_bias(j)
+                if j > BLOCK * b:
+                    finish(j - 1)
 
         def add_block(b):
             for j in range(BLOCK * b, BLOCK * (b + 1)):
@@ -255,31 +240,6 @@ def tile_pinsageconv_kernel(
                 in_=node_grouped[:].rearrange("p n t -> p (n t)"),
             )
 
-        bias_part = consts.tile([P, PACK, NODES], F32)
-
-        weight_sum = consts.tile([P, 1], F32)
-        sum_wide = consts.tile([P, P], F32)
-        bq_cols = consts.tile([P, PACK], F32)
-        sum_t_of = {}
-
-        def widen_weight_sum():
-            nc.vector.tensor_reduce(out=weight_sum[:], in_=weight[:], axis=AXIS.X, op=ALU.add)
-            nc.vector.tensor_scalar(
-                out=sum_wide[:], in0=ident_f32[:], scalar1=0.0, scalar2=weight_sum[:, 0:1],
-                op0=ALU.mult, op1=ALU.add,
-            )
-            nc.vector.tensor_copy(out=bq_cols[:], in_=bq_cols_bf[:])
-
-        def transpose_weight_sum():
-            sum_t_of[0] = psum_in.tile([P, P], F32, tag="in", name="sum_t")
-            nc.tensor.transpose(sum_t_of[0][:], sum_wide[:], ident_f32[:])
-
-        def spread_bias():
-            for t in range(PACK):
-                nc.vector.tensor_scalar_mul(
-                    out=bias_part[:, t, :], in0=sum_t_of[0][:], scalar1=bq_cols[:, t : t + 1]
-                )
-
         transpose_block(0)
         transpose_block(1)
         quantise_block(0)
@@ -289,7 +249,6 @@ def tile_pinsageconv_kernel(
                 quantise_block(step + 1)
             if step < N_BLOCKS:
                 project_block(step)
-                leak_terms(step)
             if step == N_BLOCKS - 1:
                 z2 = psum_in.tile([P, FEATS], F32, tag="in")
                 nc.tensor.matmul_mx(
@@ -305,23 +264,15 @@ def tile_pinsageconv_kernel(
                 transpose_block(step + 2)
             if step == 0:
                 transpose_node()
-            if step == 1:
-                transpose_weight_sum()
             if step < N_BLOCKS:
                 elementwise_block(step)
             if step == 0:
                 quantise_node()
-                widen_weight_sum()
-            if step == 1:
-                spread_bias()
             if step >= 1:
                 add_block(step - 1)
 
         agg_grouped = consts.tile([P, NODES, PACK], BF16, align_bytes=64)
-        nc.vector.tensor_tensor(
-            out=agg_grouped[:], in0=acc[:].rearrange("p t n -> p n t"),
-            in1=bias_part[:].rearrange("p t n -> p n t"), op=ALU.add,
-        )
+        nc.vector.tensor_copy(out=agg_grouped[:], in_=acc[:].rearrange("p t n -> p n t"))
         nc.vector.quantize_mx(
             out=concat_codes[:, 1, :].bitcast(FP8X4),
             scales=concat_scales[:, 1, :],

@@ -20,11 +20,13 @@ FEATS = 512
 PACK = 4
 PAIR = 2
 N_PAIRS = NGBRS // PAIR
-BLOCK = 4
-PAIRS_IN_BLOCK = BLOCK // PAIR
-N_BLOCKS = NGBRS // BLOCK
+BLOCKS = [4] * 8
+N_BLOCKS = len(BLOCKS)
+STARTS = [sum(BLOCKS[:b]) for b in range(N_BLOCKS)]
 NEG_SLOPE = 0.01
-KINDS = ["one", "vector", "one", "scalar", "one", "scalar", "one", "vector"]
+TINY = 1e-36
+NODE_STEP = 1
+KINDS = ["scalar","one","one","scalar","one","scalar","one","one"]
 
 FLOPS = 2 * NODES * NGBRS * FEATS * FEATS + 2 * NODES * 2 * FEATS * FEATS
 
@@ -59,7 +61,7 @@ def tile_pinsageconv_kernel(
         node_bf = consts.tile([P, FEATS], BF16)
         nc.scalar.dma_start(out=node_bf[:], in_=h_node[:, :])
 
-        nc.scalar.sqrt(out=warm[:], in_=warm[:])
+        nc.scalar.activation(out=warm[:], in_=warm[:], func=ACT.Abs_reciprocal_sqrt)
 
         ident_f32 = consts.tile([P, P], F32)
         make_identity(nc, ident_f32[:])
@@ -74,7 +76,7 @@ def tile_pinsageconv_kernel(
         ww_words = consts.tile([P, 2, FEATS], U32, align_bytes=64)
         bw_all = consts.tile([P, FEATS], BF16)
 
-        for g in range(PAIRS_IN_BLOCK):
+        for g in range(2):
             load_pair(g)
         for q in range(4):
             nc.sync.dma_start(
@@ -85,7 +87,7 @@ def tile_pinsageconv_kernel(
             out=wq_words[:].bitcast(I32),
             in_=Wq_words[0].rearrange("p n t -> p (n t)").bitcast(I32),
         )
-        for g in range(PAIRS_IN_BLOCK, N_PAIRS):
+        for g in range(2, N_PAIRS):
             load_pair(g)
         for g in range(2):
             nc.sync.dma_start(
@@ -113,11 +115,6 @@ def tile_pinsageconv_kernel(
         weight_drop = consts.tile([P, NGBRS], F32)
         nc.vector.tensor_scalar_mul(out=weight_drop[:], in0=weight[:], scalar1=NEG_SLOPE - 1.0)
 
-        bq_all = psum_z.tile([P, FEATS], F32, tag="z")
-        nc.tensor.matmul(out=bq_all[:], lhsT=ones_bf16[:], rhs=bq_row[:], start=True, stop=True)
-        bq_wide = consts.tile([P, PACK, P], F32)
-        nc.vector.tensor_copy(out=bq_wide[:], in_=bq_all[:].rearrange("p (m t) -> p t m", t=PACK))
-
         concat_codes = consts.tile([P, 2, NODES], U32, align_bytes=64)
         concat_scales = consts.tile([P, 2, NODES], U8, align_bytes=64)
         acc = psum_acc.tile([P, PACK, NODES], F32)
@@ -134,29 +131,37 @@ def tile_pinsageconv_kernel(
             for u in range(2):
                 nc.tensor.transpose(dest[:, u, :], words[:, u::2], ident_f32[:])
 
+        x_t_of = {}
+
         def transpose_block(b):
-            grouped_of[b] = stage.tile([P, BLOCK, NODES, PACK], BF16, align_bytes=64, name="grouped")
-            for q in range(PAIRS_IN_BLOCK):
-                g = PAIRS_IN_BLOCK * b + q
+            for i in range(0, BLOCKS[b], PAIR):
                 x_t = psum_in.tile([P, PAIR, 2, NODES], F32, tag="in")
-                for i in range(PAIR):
-                    transpose_words(x_t[:, i], x_tiles[g][:, i, :])
-                nc.scalar.copy(
-                    out=grouped_of[b][:, PAIR * q : PAIR * (q + 1)].bitcast(F32),
-                    in_=x_t[:].rearrange("p i u n -> p i n u"),
-                )
+                for k in range(min(PAIR, BLOCKS[b] - i)):
+                    j = STARTS[b] + i + k
+                    transpose_words(x_t[:, k], x_tiles[j // PAIR][:, j % PAIR, :])
+                x_t_of[b, i] = x_t
+
+        def collect_words(b, i):
+            if i == 0:
+                grouped_of[b] = stage.tile([P, max(BLOCKS), NODES, PACK], BF16, align_bytes=64, name="grouped")
+            m = min(PAIR, BLOCKS[b] - i)
+            nc.scalar.copy(
+                out=grouped_of[b][:, i : i + m].bitcast(F32),
+                in_=x_t_of[b, i][:, 0:m].rearrange("p i u n -> p i n u"),
+            )
 
         def quantise_block(b):
-            codes_of[b] = stage.tile([P, BLOCK * NODES], U32, align_bytes=64, name="codes")
-            scales_of[b] = stage.tile([P, BLOCK * NODES], U8, align_bytes=64, name="scales")
+            n = BLOCKS[b]
+            codes_of[b] = stage.tile([P, max(BLOCKS) * NODES], U32, align_bytes=64, name="codes")
+            scales_of[b] = stage.tile([P, max(BLOCKS) * NODES], U8, align_bytes=64, name="scales")
             nc.vector.quantize_mx(
-                out=codes_of[b][:].bitcast(FP8X4),
-                scales=scales_of[b][:],
-                in_=grouped_of[b][:].rearrange("p j n t -> p (j n t)"),
+                out=codes_of[b][:, 0 : n * NODES].bitcast(FP8X4),
+                scales=scales_of[b][:, 0 : n * NODES],
+                in_=grouped_of[b][:, 0:n].rearrange("p j n t -> p (j n t)"),
             )
 
         def project_block(b):
-            for i in range(BLOCK):
+            for i in range(BLOCKS[b]):
                 cols = slice(NODES * i, NODES * (i + 1))
                 z = psum_z.tile([P, FEATS], F32, tag="z")
                 nc.tensor.matmul_mx(
@@ -168,7 +173,7 @@ def tile_pinsageconv_kernel(
                     start=True,
                     stop=True,
                 )
-                z_of[BLOCK * b + i] = z
+                z_of[STARTS[b] + i] = z
 
         def by_word(z):
             return z[:].rearrange("p (m t) -> p t m", t=PACK)
@@ -210,20 +215,34 @@ def tile_pinsageconv_kernel(
                 terms_of[j].append(term)
 
         def elementwise_block(b):
-            for j in range(BLOCK * b, BLOCK * (b + 1) + 1):
-                if j < BLOCK * (b + 1):
-                    add_bias(j)
-                if j > BLOCK * b:
-                    finish(j - 1)
+            first, n = STARTS[b], BLOCKS[b]
+            for i in range(n + 1):
+                if i < n:
+                    add_bias(first + i)
+                if i == min(0, n - 1):
+                    if b + 1 < N_BLOCKS:
+                        quantise_block(b + 1)
+                    if b == NODE_STEP + 1:
+                        quantise_node()
+                for q, at in enumerate([0,0]):
+                    if i == min(at, n) and b + 2 < N_BLOCKS and PAIR * q < BLOCKS[b + 2]:
+                        collect_words(b + 2, PAIR * q)
+                        if q == 0 and b == NODE_STEP:
+                            collect_node()
+                if i > 0:
+                    finish(first + i - 1)
 
-        def add_block(b):
-            for j in range(BLOCK * b, BLOCK * (b + 1)):
+        added = []
+
+        def add_terms(order):
+            for j in order:
+                added.append(j)
                 for k, term in enumerate(terms_of[j]):
                     for t in range(PACK):
                         nc.tensor.matmul(
                             out=acc[:, t, :], lhsT=term[:, t, :], rhs=ident_f32[:], is_transpose=True,
-                            start=(j == 0 and t == 0),
-                            stop=(j == NGBRS - 1 and k == len(terms_of[j]) - 1 and t == PACK - 1),
+                            start=(len(added) == 1 and t == 0 and k == 0),
+                            stop=(len(added) == NGBRS and k == len(terms_of[j]) - 1 and t == PACK - 1),
                         )
 
         node_grouped = consts.tile([P, NODES, PACK], BF16, align_bytes=64)
@@ -231,6 +250,10 @@ def tile_pinsageconv_kernel(
         def transpose_node():
             node_t = psum_in.tile([P, 2, NODES], F32, tag="in")
             transpose_words(node_t, node_bf[:])
+            x_t_of["node"] = node_t
+
+        def collect_node():
+            node_t = x_t_of["node"]
             nc.scalar.copy(out=node_grouped[:].bitcast(F32), in_=node_t[:].rearrange("p u n -> p n u"))
 
         def quantise_node():
@@ -240,13 +263,19 @@ def tile_pinsageconv_kernel(
                 in_=node_grouped[:].rearrange("p n t -> p (n t)"),
             )
 
-        transpose_block(0)
-        transpose_block(1)
-        quantise_block(0)
+        for b in range(2):
+            transpose_block(b)
+            if b == 0:
+                bq_all = psum_z.tile([P, FEATS], F32, tag="z")
+                nc.tensor.matmul(out=bq_all[:], lhsT=ones_bf16[:], rhs=bq_row[:], start=True, stop=True)
+                bq_wide = consts.tile([P, PACK, P], F32)
+                nc.vector.tensor_copy(out=bq_wide[:], in_=bq_all[:].rearrange("p (m t) -> p t m", t=PACK))
+            for i in range(0, BLOCKS[b], PAIR):
+                collect_words(b, i)
+        for b in range(1):
+            quantise_block(b)
         z2 = None
         for step in range(N_BLOCKS + 1):
-            if step + 1 < N_BLOCKS:
-                quantise_block(step + 1)
             if step < N_BLOCKS:
                 project_block(step)
             if step == N_BLOCKS - 1:
@@ -262,14 +291,15 @@ def tile_pinsageconv_kernel(
                 )
             if step + 2 < N_BLOCKS:
                 transpose_block(step + 2)
-            if step == 0:
+            if step == NODE_STEP:
                 transpose_node()
+            ready = NGBRS if step == N_BLOCKS else max(0, STARTS[step] + BLOCKS[step] - 4)
+            if step == N_BLOCKS:
+                add_terms([j for j in range(NGBRS) if j not in added])
+            else:
+                add_terms(range(len(added), min(ready, STARTS[step])))
             if step < N_BLOCKS:
                 elementwise_block(step)
-            if step == 0:
-                quantise_node()
-            if step >= 1:
-                add_block(step - 1)
 
         agg_grouped = consts.tile([P, NODES, PACK], BF16, align_bytes=64)
         nc.vector.tensor_copy(out=agg_grouped[:], in_=acc[:].rearrange("p t n -> p n t"))
@@ -300,14 +330,12 @@ def tile_pinsageconv_kernel(
                 op0=ALU.mult, op1=ALU.max,
             )
             nc.scalar.activation(out=squares[:, cols], in_=h2[:, cols], func=ACT.Square, accum_out=sum_sq[i][:])
-        norm = consts.tile([P, 1], F32)
-        nc.scalar.activation(out=norm[:], in_=sum_sq[0][:], func=ACT.Sqrt, bias=sum_sq[1][:, 0:1], scale=1.0)
-        norm_den = consts.tile([P, 1], F32)
-        nc.vector.scalar_tensor_tensor(
-            out=norm_den[:], in0=norm[:], scalar=0.0, in1=norm[:], op0=ALU.is_equal, op1=ALU.add
-        )
+        sum_floor = consts.tile([P, 1], F32)
+        nc.vector.tensor_scalar_max(out=sum_floor[:], in0=sum_sq[0][:], scalar1=TINY)
         norm_inv = consts.tile([P, 1], F32)
-        nc.vector.reciprocal(out=norm_inv[:], in_=norm_den[:])
+        nc.scalar.activation(
+            out=norm_inv[:], in_=sum_sq[1][:], func=ACT.Abs_reciprocal_sqrt, bias=sum_floor[:, 0:1], scale=1.0
+        )
         result = consts.tile([P, FEATS], F32)
         for cols, queue in zip(halves, [nc.sync, nc.scalar]):
             nc.vector.tensor_scalar_mul(out=result[:, cols], in0=h2[:, cols], scalar1=norm_inv[:, 0:1])

@@ -20,13 +20,13 @@ FEATS = 512
 PACK = 4
 PAIR = 2
 N_PAIRS = NGBRS // PAIR
-BLOCKS = [4] * 8
+BLOCKS = [2, 2] + [4] * 7
 N_BLOCKS = len(BLOCKS)
 STARTS = [sum(BLOCKS[:b]) for b in range(N_BLOCKS)]
 NEG_SLOPE = 0.01
 TINY = 1e-36
-NODE_STEP = 1
-KINDS = ["scalar","one","one","scalar","one","scalar","one","one"]
+KINDS = ["oneG","two","oneS","two"]
+LAST = NGBRS - 2
 
 FLOPS = 2 * NODES * NGBRS * FEATS * FEATS + 2 * NODES * 2 * FEATS * FEATS
 
@@ -39,27 +39,27 @@ def tile_pinsageconv_kernel(
         ctx.enter_context(tc.manual_schedule())
         consts = ctx.enter_context(tc.tile_pool(name="consts", bufs=1))
         x_pool = ctx.enter_context(tc.tile_pool(name="x", bufs=N_PAIRS))
-        stage = ctx.enter_context(tc.tile_pool(name="stage", bufs=3))
+        stage = ctx.enter_context(tc.tile_pool(name="stage", bufs=4))
         mids = ctx.enter_context(tc.tile_pool(name="mids", bufs=12))
-        terms = ctx.enter_context(tc.tile_pool(name="terms", bufs=16))
-        psum_in = ctx.enter_context(tc.psum_pool(name="psum_in", bufs=3))
-        psum_z = ctx.enter_context(tc.psum_pool(name="psum_z", bufs=4))
+        terms = ctx.enter_context(tc.tile_pool(name="terms", bufs=20))
+        psum_in = ctx.enter_context(tc.psum_pool(name="psum_in", bufs=2))
+        psum_z = ctx.enter_context(tc.psum_pool(name="psum_z", bufs=5))
         psum_acc = ctx.enter_context(tc.psum_pool(name="psum_acc", bufs=1))
 
-        w_planes = consts.tile([P, 3, FEATS], U8, align_bytes=64)
-        nc.vector.memset(w_planes[:].rearrange("p w n -> p (w n)").bitcast(I32), 0)
+        wq_plane = consts.tile([P, FEATS], U8, align_bytes=64)
+        nc.vector.memset(wq_plane[:].bitcast(I32), 0)
+        warm = consts.tile([P, 1], F32)
+        nc.vector.memset(warm[:], 1.0)
         bq_row = consts.tile([P, FEATS], BF16)
         nc.vector.memset(bq_row[:], 0.0)
         ones_bf16 = consts.tile([P, P], BF16)
         nc.vector.memset(ones_bf16[:], 1.0)
-        warm = consts.tile([P, 1], F32)
-        nc.vector.memset(warm[:], 1.0)
+        ww_planes = consts.tile([P, 2, FEATS], U8, align_bytes=64)
+        nc.vector.memset(ww_planes[:].rearrange("p w n -> p (w n)").bitcast(I32), 0)
 
         alpha_bf = consts.tile([P, NGBRS], BF16)
         nc.scalar.dma_start(out=alpha_bf[:], in_=alpha.rearrange("n k o -> n (k o)"))
         nc.scalar.dma_start(out=bq_row[0:1, :], in_=bq.rearrange("(o f) -> o f", o=1))
-        node_bf = consts.tile([P, FEATS], BF16)
-        nc.scalar.dma_start(out=node_bf[:], in_=h_node[:, :])
 
         nc.scalar.activation(out=warm[:], in_=warm[:], func=ACT.Abs_reciprocal_sqrt)
 
@@ -72,33 +72,33 @@ def tile_pinsageconv_kernel(
             x_tiles[g] = x_pool.tile([P, PAIR, FEATS], BF16, name="x")
             nc.sync.dma_start(out=x_tiles[g][:], in_=h_ngbrs[:, PAIR * g : PAIR * (g + 1), :])
 
-        wq_words = consts.tile([P, FEATS], U32, align_bytes=64)
-        ww_words = consts.tile([P, 2, FEATS], U32, align_bytes=64)
-        bw_all = consts.tile([P, FEATS], BF16)
-
-        for g in range(2):
-            load_pair(g)
-        for q in range(4):
-            nc.sync.dma_start(
-                out=w_planes[32 * q : 32 * q + 4, 0, :].bitcast(I32),
-                in_=Wq_scales[0, 4 * q : 4 * q + 4, :].bitcast(I32),
-            )
-        nc.sync.dma_start(
-            out=wq_words[:].bitcast(I32),
-            in_=Wq_words[0].rearrange("p n t -> p (n t)").bitcast(I32),
-        )
-        for g in range(2, N_PAIRS):
-            load_pair(g)
-        for g in range(2):
-            nc.sync.dma_start(
-                out=ww_words[:, g, :].bitcast(I32),
-                in_=Ww_words[g].rearrange("p n t -> p (n t)").bitcast(I32),
-            )
+        def load_plane(plane, source):
             for q in range(4):
                 nc.sync.dma_start(
-                    out=w_planes[32 * q : 32 * q + 4, 1 + g, :].bitcast(I32),
-                    in_=Ww_scales[g, 4 * q : 4 * q + 4, :].bitcast(I32),
+                    out=plane[32 * q : 32 * q + 4, :].bitcast(I32), in_=source[4 * q : 4 * q + 4, :].bitcast(I32)
                 )
+
+        def load_words(words, source):
+            nc.sync.dma_start(
+                out=words.bitcast(I32), in_=source.rearrange("p n t -> p (n t)").bitcast(I32)
+            )
+
+        wq_words = consts.tile([P, FEATS], U32, align_bytes=64)
+        ww_words = consts.tile([P, 2, FEATS], U32, align_bytes=64)
+        node_bf = consts.tile([P, FEATS], BF16)
+        bw_all = consts.tile([P, FEATS], BF16)
+
+        for g in range(1):
+            load_pair(g)
+        load_plane(wq_plane, Wq_scales[0])
+        load_words(wq_words[:], Wq_words[0])
+        for g in range(1, N_PAIRS):
+            if g == 4:
+                nc.sync.dma_start(out=node_bf[:], in_=h_node[:, :])
+            load_pair(g)
+        for g in range(2):
+            load_words(ww_words[:, g, :], Ww_words[g])
+            load_plane(ww_planes[:, g, :], Ww_scales[g])
         nc.sync.dma_start(out=bw_all[:], in_=bw.partition_broadcast(P))
 
         alpha_sum = consts.tile([P, 1], F32)
@@ -112,13 +112,17 @@ def tile_pinsageconv_kernel(
         nc.vector.reciprocal(out=alpha_inv[:], in_=alpha_den[:])
         weight = consts.tile([P, NGBRS], F32)
         nc.vector.tensor_scalar_mul(out=weight[:], in0=alpha_bf[:], scalar1=alpha_inv[:, 0:1])
-        weight_drop = consts.tile([P, NGBRS], F32)
-        nc.vector.tensor_scalar_mul(out=weight_drop[:], in0=weight[:], scalar1=NEG_SLOPE - 1.0)
+        weight_sum = consts.tile([P, 1], F32)
+        nc.vector.tensor_scalar_mul(out=weight_sum[:], in0=alpha_sum[:], scalar1=alpha_inv[:, 0:1])
+        weight_slope = consts.tile([P, NGBRS], F32)
+        nc.vector.tensor_scalar_mul(out=weight_slope[:], in0=weight[:], scalar1=NEG_SLOPE)
 
         concat_codes = consts.tile([P, 2, NODES], U32, align_bytes=64)
         concat_scales = consts.tile([P, 2, NODES], U8, align_bytes=64)
         acc = psum_acc.tile([P, PACK, NODES], F32)
 
+        x_t_of = {}
+        sorted_of = {}
         grouped_of = {}
         codes_of = {}
         scales_of = {}
@@ -126,19 +130,19 @@ def tile_pinsageconv_kernel(
         mid_of = {}
         terms_of = {}
 
-        def transpose_words(dest, rows):
-            words = rows.bitcast(F32)
-            for u in range(2):
-                nc.tensor.transpose(dest[:, u, :], words[:, u::2], ident_f32[:])
+        def by_word(z):
+            return z[:].rearrange("p (m t) -> p t m", t=PACK)
 
-        x_t_of = {}
+        def transpose_words(dest, words, u):
+            nc.tensor.transpose(dest, words.bitcast(F32)[:, u::2], ident_f32[:])
 
         def transpose_block(b):
             for i in range(0, BLOCKS[b], PAIR):
                 x_t = psum_in.tile([P, PAIR, 2, NODES], F32, tag="in")
                 for k in range(min(PAIR, BLOCKS[b] - i)):
-                    j = STARTS[b] + i + k
-                    transpose_words(x_t[:, k], x_tiles[j // PAIR][:, j % PAIR, :])
+                    g, row = divmod(STARTS[b] + i + k, PAIR)
+                    for u in range(2):
+                        transpose_words(x_t[:, k, u, :], x_tiles[g][:, row, :], u)
                 x_t_of[b, i] = x_t
 
         def collect_words(b, i):
@@ -169,91 +173,102 @@ def tile_pinsageconv_kernel(
                     lhsT=codes_of[b][:, cols].bitcast(FP8X4),
                     lhsT_scale=scales_of[b][:, cols],
                     rhs=wq_words[:].bitcast(FP8X4),
-                    rhs_scale=w_planes[:, 0, :],
+                    rhs_scale=wq_plane[:],
                     start=True,
                     stop=True,
                 )
                 z_of[STARTS[b] + i] = z
 
-        def by_word(z):
-            return z[:].rearrange("p (m t) -> p t m", t=PACK)
+        def kind(j):
+            return KINDS[j % len(KINDS)]
 
-        def weighted(source, j):
+        def new_term(j):
             term = terms.tile([P, PACK, P], F32, name="term")
-            nc.scalar.activation(out=term[:], in_=source[:], func=ACT.Copy, scale=weight[:, j : j + 1])
             terms_of[j].append(term)
+            return term
 
-        def add_bias(j):
-            mid_of[j] = mids.tile([P, PACK, P], F32, name="mid")
-            nc.vector.tensor_tensor(out=mid_of[j][:], in0=by_word(z_of[j]), in1=bq_wide[:], op=ALU.add)
+        def weigh_rest(engine, j):
+            engine.tensor_scalar(
+                out=new_term(j)[:], in0=mid_of[j][:], scalar1=weight[:, j : j + 1], scalar2=1.0 - NEG_SLOPE,
+                op0=ALU.mult, op1=ALU.mult,
+            )
+
+        def begin(j):
             terms_of[j] = []
-            if KINDS[j % 8] != "one":
-                weighted(mid_of[j], j)
+            mid = mids.tile([P, PACK, P], F32, name="mid")
+            mid_of[j] = mid
+            z = by_word(z_of[j])
+            if kind(j) == "two":
+                nc.vector.tensor_tensor(out=mid[:], in0=z, in1=bq_neg[:], op=ALU.max)
+                nc.scalar.activation(out=new_term(j)[:], in_=z, func=ACT.Copy, scale=weight_slope[:, j : j + 1])
+                if j != NGBRS - 1:
+                    weigh_rest(nc.gpsimd, j)
+            elif j != LAST:
+                nc.vector.scalar_tensor_tensor(
+                    out=mid[:], in0=z, scalar=NEG_SLOPE, in1=bq_low[:], op0=ALU.mult, op1=ALU.add
+                )
 
         def finish(j):
-            u = mid_of[j]
-            if KINDS[j % 8] == "one":
-                nc.vector.scalar_tensor_tensor(
-                    out=u[:], in0=u[:], scalar=NEG_SLOPE, in1=u[:], op0=ALU.mult, op1=ALU.max
-                )
-                weighted(u, j)
-            elif KINDS[j % 8] == "vector":
-                term = terms.tile([P, PACK, P], F32, name="term")
-                nc.vector.tensor_scalar(
-                    out=term[:], in0=u[:], scalar1=0.0, scalar2=weight_drop[:, j : j + 1],
-                    op0=ALU.min, op1=ALU.mult,
-                )
-                terms_of[j].append(term)
+            if kind(j) == "two" or j == LAST:
+                return
+            mid = mid_of[j]
+            nc.vector.tensor_tensor(out=mid[:], in0=by_word(z_of[j]), in1=mid[:], op=ALU.max)
+            if kind(j) == "oneS" or j >= STARTS[-1]:
+                nc.scalar.activation(out=new_term(j)[:], in_=mid[:], func=ACT.Copy, scale=weight[:, j : j + 1])
             else:
-                below = mids.tile([P, PACK, P], F32, name="mid")
-                nc.scalar.activation(out=below[:], in_=u[:], func=ACT.Relu, scale=-1.0)
-                term = terms.tile([P, PACK, P], F32, name="term")
                 nc.gpsimd.tensor_scalar(
-                    out=term[:], in0=below[:], scalar1=weight[:, j : j + 1], scalar2=1.0 - NEG_SLOPE,
+                    out=new_term(j)[:], in0=mid[:], scalar1=weight[:, j : j + 1], scalar2=1.0,
                     op0=ALU.mult, op1=ALU.mult,
                 )
-                terms_of[j].append(term)
+
+        def finish_last(j):
+            z, mid, term = by_word(z_of[j]), mid_of[j], new_term(j)
+            halves = [slice(0, PACK // 2), slice(PACK // 2, PACK)]
+            for t in halves:
+                nc.vector.scalar_tensor_tensor(
+                    out=mid[:, t], in0=z[:, t], scalar=NEG_SLOPE, in1=bq_low[:, t], op0=ALU.mult, op1=ALU.add
+                )
+            weigh_rest(nc.vector, NGBRS - 1)
+            for t in halves:
+                nc.vector.tensor_tensor(out=mid[:, t], in0=z[:, t], in1=mid[:, t], op=ALU.max)
+            for t in halves:
+                nc.vector.tensor_scalar_mul(out=term[:, t], in0=mid[:, t], scalar1=weight[:, j : j + 1])
 
         def elementwise_block(b):
             first, n = STARTS[b], BLOCKS[b]
             for i in range(n + 1):
                 if i < n:
-                    add_bias(first + i)
-                if i == min(0, n - 1):
+                    begin(first + i)
+                if i == (n - 1 if b == 0 else 0):
                     if b + 1 < N_BLOCKS:
                         quantise_block(b + 1)
-                    if b == NODE_STEP + 1:
+                    if b == 1:
                         quantise_node()
                 for q, at in enumerate([0,0]):
                     if i == min(at, n) and b + 2 < N_BLOCKS and PAIR * q < BLOCKS[b + 2]:
                         collect_words(b + 2, PAIR * q)
-                        if q == 0 and b == NODE_STEP:
-                            collect_node()
                 if i > 0:
                     finish(first + i - 1)
 
-        added = []
+        n_sums = 1 + sum(2 if kind(j) == "two" else 1 for j in range(NGBRS))
+        summed = []
 
-        def add_terms(order):
-            for j in order:
-                added.append(j)
-                for k, term in enumerate(terms_of[j]):
+        def sum_terms(js):
+            for j in js:
+                for term in terms_of[j]:
+                    summed.append(term)
                     for t in range(PACK):
                         nc.tensor.matmul(
                             out=acc[:, t, :], lhsT=term[:, t, :], rhs=ident_f32[:], is_transpose=True,
-                            start=(len(added) == 1 and t == 0 and k == 0),
-                            stop=(len(added) == NGBRS and k == len(terms_of[j]) - 1 and t == PACK - 1),
+                            start=(len(summed) == 1 and t == 0), stop=(len(summed) == n_sums and t == PACK - 1),
                         )
 
         node_grouped = consts.tile([P, NODES, PACK], BF16, align_bytes=64)
 
         def transpose_node():
-            node_t = psum_in.tile([P, 2, NODES], F32, tag="in")
-            transpose_words(node_t, node_bf[:])
-            x_t_of["node"] = node_t
-
-        def collect_node():
-            node_t = x_t_of["node"]
+            node_t = psum_z.tile([P, 2, NODES], F32, tag="z")
+            for u in range(2):
+                transpose_words(node_t[:, u, :], node_bf[:], u)
             nc.scalar.copy(out=node_grouped[:].bitcast(F32), in_=node_t[:].rearrange("p u n -> p n u"))
 
         def quantise_node():
@@ -263,17 +278,20 @@ def tile_pinsageconv_kernel(
                 in_=node_grouped[:].rearrange("p n t -> p (n t)"),
             )
 
-        for b in range(2):
-            transpose_block(b)
-            if b == 0:
-                bq_all = psum_z.tile([P, FEATS], F32, tag="z")
-                nc.tensor.matmul(out=bq_all[:], lhsT=ones_bf16[:], rhs=bq_row[:], start=True, stop=True)
-                bq_wide = consts.tile([P, PACK, P], F32)
-                nc.vector.tensor_copy(out=bq_wide[:], in_=bq_all[:].rearrange("p (m t) -> p t m", t=PACK))
-            for i in range(0, BLOCKS[b], PAIR):
-                collect_words(b, i)
-        for b in range(1):
-            quantise_block(b)
+        transpose_block(0)
+        bq_all = psum_z.tile([P, FEATS], F32, tag="z")
+        nc.tensor.matmul(out=bq_all[:], lhsT=ones_bf16[:], rhs=bq_row[:], start=True, stop=True)
+        collect_words(0, 0)
+        bq_low = consts.tile([P, PACK, P], F32)
+        nc.scalar.mul(out=bq_low[:], in_=by_word(bq_all), mul=NEG_SLOPE - 1.0)
+        bq_neg = consts.tile([P, PACK, P], F32)
+        nc.scalar.mul(out=bq_neg[:], in_=by_word(bq_all), mul=-1.0)
+        quantise_block(0)
+        bias_term = consts.tile([P, PACK, P], F32)
+        nc.gpsimd.tensor_scalar(
+            out=bias_term[:], in0=bq_neg[:], scalar1=weight_sum[:, 0:1], scalar2=-1.0, op0=ALU.mult, op1=ALU.mult
+        )
+        terms_of["bias"] = [bias_term]
         z2 = None
         for step in range(N_BLOCKS + 1):
             if step < N_BLOCKS:
@@ -285,21 +303,28 @@ def tile_pinsageconv_kernel(
                     lhsT=concat_codes[:, 0, :].bitcast(FP8X4),
                     lhsT_scale=concat_scales[:, 0, :],
                     rhs=ww_words[:, 0, :].bitcast(FP8X4),
-                    rhs_scale=w_planes[:, 1, :],
+                    rhs_scale=ww_planes[:, 0, :],
                     start=True,
                     stop=False,
                 )
+            if step == 0:
+                transpose_block(1)
+                for i in range(0, BLOCKS[1], PAIR):
+                    collect_words(1, i)
+                transpose_node()
             if step + 2 < N_BLOCKS:
                 transpose_block(step + 2)
-            if step == NODE_STEP:
-                transpose_node()
-            ready = NGBRS if step == N_BLOCKS else max(0, STARTS[step] + BLOCKS[step] - 4)
+            if step == 1:
+                sum_terms(["bias"])
+            if step >= 1:
+                block = range(STARTS[step - 1], STARTS[step - 1] + BLOCKS[step - 1])
+                sum_terms(sorted([j for j in block if j != LAST], key=lambda j: (j >= STARTS[-1] and kind(j) != "two")))
             if step == N_BLOCKS:
-                add_terms([j for j in range(NGBRS) if j not in added])
-            else:
-                add_terms(range(len(added), min(ready, STARTS[step])))
+                sum_terms([LAST])
             if step < N_BLOCKS:
                 elementwise_block(step)
+            if step == N_BLOCKS - 1:
+                finish_last(LAST)
 
         agg_grouped = consts.tile([P, NODES, PACK], BF16, align_bytes=64)
         nc.vector.tensor_copy(out=agg_grouped[:], in_=acc[:].rearrange("p t n -> p n t"))
@@ -313,7 +338,7 @@ def tile_pinsageconv_kernel(
             lhsT=concat_codes[:, 1, :].bitcast(FP8X4),
             lhsT_scale=concat_scales[:, 1, :],
             rhs=ww_words[:, 1, :].bitcast(FP8X4),
-            rhs_scale=w_planes[:, 2, :],
+            rhs_scale=ww_planes[:, 1, :],
             start=False,
             stop=True,
         )

@@ -46,12 +46,12 @@ def tile_pinsageconv_kernel(
         psum_z = ctx.enter_context(tc.psum_pool(name="psum_z", bufs=5))
         psum_acc = ctx.enter_context(tc.psum_pool(name="psum_acc", bufs=1))
 
+        bq_row = consts.tile([P, FEATS], BF16)
+        nc.vector.memset(bq_row[:].bitcast(I32), 0)
         wq_plane = consts.tile([P, FEATS], U8, align_bytes=64)
         nc.vector.memset(wq_plane[:].bitcast(I32), 0)
         warm = consts.tile([P, 1], F32)
         nc.vector.memset(warm[:], 1.0)
-        bq_row = consts.tile([P, FEATS], BF16)
-        nc.vector.memset(bq_row[:], 0.0)
         ones_bf16 = consts.tile([P, P], BF16)
         nc.vector.memset(ones_bf16[:], 1.0)
         ww_planes = consts.tile([P, 2, FEATS], U8, align_bytes=64)
@@ -88,11 +88,11 @@ def tile_pinsageconv_kernel(
         node_bf = consts.tile([P, FEATS], BF16)
         bw_all = consts.tile([P, FEATS], BF16)
 
-        for g in range(1):
+        for g in range(2):
             load_pair(g)
         load_plane(wq_plane, Wq_scales[0])
         load_words(wq_words[:], Wq_words[0])
-        for g in range(1, N_PAIRS):
+        for g in range(2, N_PAIRS):
             if g == 4:
                 nc.sync.dma_start(out=node_bf[:], in_=h_node[:, :])
             load_pair(g)
@@ -137,9 +137,10 @@ def tile_pinsageconv_kernel(
             nc.tensor.transpose(dest, words.bitcast(F32)[:, u::2], ident_f32[:])
 
         def transpose_block(b):
-            for i in range(0, BLOCKS[b], PAIR):
+            step = 1 if b == 0 else PAIR
+            for i in range(0, BLOCKS[b], step):
                 x_t = psum_in.tile([P, PAIR, 2, NODES], F32, tag="in")
-                for k in range(min(PAIR, BLOCKS[b] - i)):
+                for k in range(min(step, BLOCKS[b] - i)):
                     g, row = divmod(STARTS[b] + i + k, PAIR)
                     for u in range(2):
                         transpose_words(x_t[:, k, u, :], x_tiles[g][:, row, :], u)
@@ -148,11 +149,13 @@ def tile_pinsageconv_kernel(
         def collect_words(b, i):
             if i == 0:
                 grouped_of[b] = stage.tile([P, max(BLOCKS), NODES, PACK], BF16, align_bytes=64, name="grouped")
-            m = min(PAIR, BLOCKS[b] - i)
-            nc.scalar.copy(
-                out=grouped_of[b][:, i : i + m].bitcast(F32),
-                in_=x_t_of[b, i][:, 0:m].rearrange("p i u n -> p i n u"),
-            )
+            m = 1 if b == 0 else min(PAIR, BLOCKS[b] - i)
+            out_words = grouped_of[b][:, i : i + m].bitcast(F32)
+            in_words = x_t_of[b, i][:, 0:m].rearrange("p i u n -> p i n u")
+            if b == 0 and i == 1:
+                nc.vector.tensor_copy(out=out_words, in_=in_words)
+            else:
+                nc.scalar.copy(out=out_words, in_=in_words)
 
         def quantise_block(b):
             n = BLOCKS[b]
@@ -239,10 +242,10 @@ def tile_pinsageconv_kernel(
             for i in range(n + 1):
                 if i < n:
                     begin(first + i)
-                if i == (n - 1 if b == 0 else 0):
+                if i == 0:
                     if b + 1 < N_BLOCKS:
                         quantise_block(b + 1)
-                    if b == 1:
+                    if b == 2:
                         quantise_node()
                 for q, at in enumerate([0,0]):
                     if i == min(at, n) and b + 2 < N_BLOCKS and PAIR * q < BLOCKS[b + 2]:
@@ -281,9 +284,13 @@ def tile_pinsageconv_kernel(
         transpose_block(0)
         bq_all = psum_z.tile([P, FEATS], F32, tag="z")
         nc.tensor.matmul(out=bq_all[:], lhsT=ones_bf16[:], rhs=bq_row[:], start=True, stop=True)
-        collect_words(0, 0)
+        for i in range(BLOCKS[0]):
+            collect_words(0, i)
         bq_low = consts.tile([P, PACK, P], F32)
         nc.scalar.mul(out=bq_low[:], in_=by_word(bq_all), mul=NEG_SLOPE - 1.0)
+        transpose_block(1)
+        for i in range(0, BLOCKS[1], PAIR):
+            collect_words(1, i)
         bq_neg = consts.tile([P, PACK, P], F32)
         nc.scalar.mul(out=bq_neg[:], in_=by_word(bq_all), mul=-1.0)
         quantise_block(0)
@@ -296,7 +303,7 @@ def tile_pinsageconv_kernel(
         for step in range(N_BLOCKS + 1):
             if step < N_BLOCKS:
                 project_block(step)
-            if step == N_BLOCKS - 1:
+            if step == N_BLOCKS - 2:
                 z2 = psum_in.tile([P, FEATS], F32, tag="in")
                 nc.tensor.matmul_mx(
                     out=z2[:],
@@ -307,17 +314,14 @@ def tile_pinsageconv_kernel(
                     start=True,
                     stop=False,
                 )
-            if step == 0:
-                transpose_block(1)
-                for i in range(0, BLOCKS[1], PAIR):
-                    collect_words(1, i)
+            if step == 1:
                 transpose_node()
             if step + 2 < N_BLOCKS:
                 transpose_block(step + 2)
-            if step == 1:
+            if step == 2:
                 sum_terms(["bias"])
-            if step >= 1:
-                block = range(STARTS[step - 1], STARTS[step - 1] + BLOCKS[step - 1])
+            if step >= 2:
+                block = range(STARTS[step - 1] if step > 2 else 0, STARTS[step - 1] + BLOCKS[step - 1])
                 sum_terms(sorted([j for j in block if j != LAST], key=lambda j: (j >= STARTS[-1] and kind(j) != "two")))
             if step == N_BLOCKS:
                 sum_terms([LAST])

@@ -54,6 +54,8 @@ def tile_pinsageconv_kernel(
         nc.vector.memset(warm[:], 1.0)
         ones_bf16 = consts.tile([P, P], BF16)
         nc.vector.memset(ones_bf16[:], 1.0)
+        warm_row = consts.tile([P, FEATS], BF16)
+        nc.vector.memset(warm_row[:], 0.0)
         ww_planes = consts.tile([P, 2, FEATS], U8, align_bytes=64)
         nc.vector.memset(ww_planes[:].rearrange("p w n -> p (w n)").bitcast(I32), 0)
 
@@ -281,6 +283,9 @@ def tile_pinsageconv_kernel(
                 in_=node_grouped[:].rearrange("p n t -> p (n t)"),
             )
 
+        for i in range(2):
+            idle = psum_z.tile([P, FEATS], F32, tag="z")
+            nc.tensor.matmul(out=idle[:], lhsT=ones_bf16[:], rhs=warm_row[:], start=True, stop=True)
         transpose_block(0)
         bq_all = psum_z.tile([P, FEATS], F32, tag="z")
         nc.tensor.matmul(out=bq_all[:], lhsT=ones_bf16[:], rhs=bq_row[:], start=True, stop=True)
@@ -299,21 +304,28 @@ def tile_pinsageconv_kernel(
             out=bias_term[:], in0=bq_neg[:], scalar1=weight_sum[:, 0:1], scalar2=-1.0, op0=ALU.mult, op1=ALU.mult
         )
         terms_of["bias"] = [bias_term]
-        z2 = None
+        halves = [slice(0, FEATS // 2), slice(FEATS // 2, FEATS)]
+        z2_of = []
+
+        def second_pass(i, cols, part):
+            nc.tensor.matmul_mx(
+                out=z2_of[i][:],
+                lhsT=concat_codes[:, part, :].bitcast(FP8X4),
+                lhsT_scale=concat_scales[:, part, :],
+                rhs=ww_words[:, part, cols].bitcast(FP8X4),
+                rhs_scale=ww_planes[:, part, cols],
+                start=(part == 0),
+                stop=(part == 1),
+            )
+
         for step in range(N_BLOCKS + 1):
             if step < N_BLOCKS:
                 project_block(step)
             if step == N_BLOCKS - 2:
-                z2 = psum_in.tile([P, FEATS], F32, tag="in")
-                nc.tensor.matmul_mx(
-                    out=z2[:],
-                    lhsT=concat_codes[:, 0, :].bitcast(FP8X4),
-                    lhsT_scale=concat_scales[:, 0, :],
-                    rhs=ww_words[:, 0, :].bitcast(FP8X4),
-                    rhs_scale=ww_planes[:, 0, :],
-                    start=True,
-                    stop=False,
-                )
+                for i, cols in enumerate(halves):
+                    z2 = psum_in.tile([P, FEATS // 2], F32, tag="in")
+                    z2_of.append(z2)
+                    second_pass(i, cols, 0)
             if step == 1:
                 transpose_node()
             if step + 2 < N_BLOCKS:
@@ -331,28 +343,23 @@ def tile_pinsageconv_kernel(
                 finish_last(LAST)
 
         agg_grouped = consts.tile([P, NODES, PACK], BF16, align_bytes=64)
-        nc.vector.tensor_copy(out=agg_grouped[:], in_=acc[:].rearrange("p t n -> p n t"))
-        nc.vector.quantize_mx(
-            out=concat_codes[:, 1, :].bitcast(FP8X4),
-            scales=concat_scales[:, 1, :],
-            in_=agg_grouped[:].rearrange("p n t -> p (n t)"),
-        )
-        nc.tensor.matmul_mx(
-            out=z2[:],
-            lhsT=concat_codes[:, 1, :].bitcast(FP8X4),
-            lhsT_scale=concat_scales[:, 1, :],
-            rhs=ww_words[:, 1, :].bitcast(FP8X4),
-            rhs_scale=ww_planes[:, 1, :],
-            start=False,
-            stop=True,
-        )
-        halves = [slice(0, FEATS // 2), slice(FEATS // 2, FEATS)]
+        node_halves = [slice(0, NODES // 2), slice(NODES // 2, NODES)]
+        for rows in node_halves:
+            nc.vector.tensor_copy(out=agg_grouped[:, rows, :], in_=acc[:, :, rows].rearrange("p t n -> p n t"))
+        for rows in node_halves:
+            nc.vector.quantize_mx(
+                out=concat_codes[:, 1, rows].bitcast(FP8X4),
+                scales=concat_scales[:, 1, rows],
+                in_=agg_grouped[:, rows, :].rearrange("p n t -> p (n t)"),
+            )
+        for i, cols in enumerate(halves):
+            second_pass(i, cols, 1)
         biased2 = consts.tile([P, FEATS], F32)
         h2 = consts.tile([P, FEATS], F32)
         squares = consts.tile([P, FEATS], F32)
         sum_sq = [consts.tile([P, 1], F32, name="sum_sq%d" % i) for i in range(2)]
-        for cols in halves:
-            nc.vector.tensor_tensor(out=biased2[:, cols], in0=z2[:, cols], in1=bw_all[:, cols], op=ALU.add)
+        for i, cols in enumerate(halves):
+            nc.vector.tensor_tensor(out=biased2[:, cols], in0=z2_of[i][:], in1=bw_all[:, cols], op=ALU.add)
         for i, cols in enumerate(halves):
             nc.vector.scalar_tensor_tensor(
                 out=h2[:, cols], in0=biased2[:, cols], scalar=NEG_SLOPE, in1=biased2[:, cols],

from contextlib import ExitStack

import concourse.mybir as mybir
from concourse.masks import make_identity

F32 = mybir.dt.float32
BF16 = mybir.dt.bfloat16
I32 = mybir.dt.int32
U32 = mybir.dt.uint32
U8 = mybir.dt.uint8
FP8X4 = mybir.dt.float8_e4m3fn_x4
ALU = mybir.AluOpType
ACT = mybir.ActivationFunctionType
AXIS = mybir.AxisListType

P = 128
NODES = 128
NGBRS = 32
FEATS = 512
PACK = 4
PAIR = 2
N_PAIRS = NGBRS // PAIR
BLOCKS = [2, 2] + [4] * 7
N_BLOCKS = len(BLOCKS)
STARTS = [sum(BLOCKS[:b]) for b in range(N_BLOCKS)]
NEG_SLOPE = 0.01
TINY = 1e-36
KINDS = ["oneG","two","oneS","two"]
LAST = NGBRS - 2

FLOPS = 2 * NODES * NGBRS * FEATS * FEATS + 2 * NODES * 2 * FEATS * FEATS


def tile_pinsageconv_kernel(
    tc, h_node, h_ngbrs, alpha, Wq_words, Wq_scales, bq, Ww_words, Ww_scales, bw, out
):
    nc = tc.nc
    with ExitStack() as ctx:
        ctx.enter_context(tc.manual_schedule())
        consts = ctx.enter_context(tc.tile_pool(name="consts", bufs=1))
        x_pool = ctx.enter_context(tc.tile_pool(name="x", bufs=N_PAIRS))
        stage = ctx.enter_context(tc.tile_pool(name="stage", bufs=4))
        mids = ctx.enter_context(tc.tile_pool(name="mids", bufs=12))
        terms = ctx.enter_context(tc.tile_pool(name="terms", bufs=20))
        psum_in = ctx.enter_context(tc.psum_pool(name="psum_in", bufs=2))
        psum_z = ctx.enter_context(tc.psum_pool(name="psum_z", bufs=5))
        psum_acc = ctx.enter_context(tc.psum_pool(name="psum_acc", bufs=1))

        bq_row = consts.tile([P, FEATS], BF16)
        nc.vector.memset(bq_row[:].bitcast(I32), 0)
        wq_plane = consts.tile([P, FEATS], U8, align_bytes=64)
        nc.vector.memset(wq_plane[:].bitcast(I32), 0)
        warm = consts.tile([P, 1], F32)
        nc.vector.memset(warm[:], 1.0)
        ones_bf16 = consts.tile([P, P], BF16)
        nc.vector.memset(ones_bf16[:], 1.0)
        warm_row = consts.tile([P, FEATS], BF16)
        nc.vector.memset(warm_row[:], 0.0)
        ww_planes = consts.tile([P, 2, FEATS], U8, align_bytes=64)
        nc.vector.memset(ww_planes[:].rearrange("p w n -> p (w n)").bitcast(I32), 0)

        alpha_bf = consts.tile([P, NGBRS], BF16)
        nc.scalar.dma_start(out=alpha_bf[:], in_=alpha.rearrange("n k o -> n (k o)"))
        nc.scalar.dma_start(out=bq_row[0:1, :], in_=bq.rearrange("(o f) -> o f", o=1))

        nc.scalar.activation(out=warm[:], in_=warm[:], func=ACT.Abs_reciprocal_sqrt)

        ident_f32 = consts.tile([P, P], F32)
        make_identity(nc, ident_f32[:])

        x_tiles = {}

        def load_pair(g):
            x_tiles[g] = x_pool.tile([P, PAIR, FEATS], BF16, name="x")
            nc.sync.dma_start(out=x_tiles[g][:], in_=h_ngbrs[:, PAIR * g : PAIR * (g + 1), :])

        def load_plane(plane, source):
            for q in range(4):
                nc.sync.dma_start(
                    out=plane[32 * q : 32 * q + 4, :].bitcast(I32), in_=source[4 * q : 4 * q + 4, :].bitcast(I32)
                )

        def load_words(words, source):
            nc.sync.dma_start(
                out=words.bitcast(I32), in_=source.rearrange("p n t -> p (n t)").bitcast(I32)
            )

        wq_words = consts.tile([P, FEATS], U32, align_bytes=64)
        ww_words = consts.tile([P, 2, FEATS], U32, align_bytes=64)
        node_bf = consts.tile([P, FEATS], BF16)
        bw_all = consts.tile([P, FEATS], BF16)

        for g in range(2):
            load_pair(g)
        load_plane(wq_plane, Wq_scales[0])
        load_words(wq_words[:], Wq_words[0])
        for g in range(2, N_PAIRS):
            if g == 4:
                nc.sync.dma_start(out=node_bf[:], in_=h_node[:, :])
            load_pair(g)
        for g in range(2):
            load_words(ww_words[:, g, :], Ww_words[g])
            load_plane(ww_planes[:, g, :], Ww_scales[g])
        nc.sync.dma_start(out=bw_all[:], in_=bw.partition_broadcast(P))

        alpha_sum = consts.tile([P, 1], F32)
        nc.vector.tensor_reduce(out=alpha_sum[:], in_=alpha_bf[:], axis=AXIS.X, op=ALU.add)
        alpha_den = consts.tile([P, 1], F32)
        nc.vector.scalar_tensor_tensor(
            out=alpha_den[:], in0=alpha_sum[:], scalar=0.0, in1=alpha_sum[:],
            op0=ALU.is_equal, op1=ALU.add,
        )
        alpha_inv = consts.tile([P, 1], F32)
        nc.vector.reciprocal(out=alpha_inv[:], in_=alpha_den[:])
        weight = consts.tile([P, NGBRS], F32)
        nc.vector.tensor_scalar_mul(out=weight[:], in0=alpha_bf[:], scalar1=alpha_inv[:, 0:1])
        weight_sum = consts.tile([P, 1], F32)
        nc.vector.tensor_scalar_mul(out=weight_sum[:], in0=alpha_sum[:], scalar1=alpha_inv[:, 0:1])
        weight_slope = consts.tile([P, NGBRS], F32)
        nc.vector.tensor_scalar_mul(out=weight_slope[:], in0=weight[:], scalar1=NEG_SLOPE)

        concat_codes = consts.tile([P, 2, NODES], U32, align_bytes=64)
        concat_scales = consts.tile([P, 2, NODES], U8, align_bytes=64)
        acc = psum_acc.tile([P, PACK, NODES], F32)

        x_t_of = {}
        sorted_of = {}
        grouped_of = {}
        codes_of = {}
        scales_of = {}
        z_of = {}
        mid_of = {}
        terms_of = {}

        def by_word(z):
            return z[:].rearrange("p (m t) -> p t m", t=PACK)

        def transpose_words(dest, words, u):
            nc.tensor.transpose(dest, words.bitcast(F32)[:, u::2], ident_f32[:])

        def transpose_block(b):
            step = 1 if b == 0 else PAIR
            for i in range(0, BLOCKS[b], step):
                x_t = psum_in.tile([P, PAIR, 2, NODES], F32, tag="in")
                for k in range(min(step, BLOCKS[b] - i)):
                    g, row = divmod(STARTS[b] + i + k, PAIR)
                    for u in range(2):
                        transpose_words(x_t[:, k, u, :], x_tiles[g][:, row, :], u)
                x_t_of[b, i] = x_t

        def collect_words(b, i):
            if i == 0:
                grouped_of[b] = stage.tile([P, max(BLOCKS), NODES, PACK], BF16, align_bytes=64, name="grouped")
            m = 1 if b == 0 else min(PAIR, BLOCKS[b] - i)
            out_words = grouped_of[b][:, i : i + m].bitcast(F32)
            in_words = x_t_of[b, i][:, 0:m].rearrange("p i u n -> p i n u")
            if b == 0 and i == 1:
                nc.vector.tensor_copy(out=out_words, in_=in_words)
            else:
                nc.scalar.copy(out=out_words, in_=in_words)

        def quantise_block(b):
            n = BLOCKS[b]
            codes_of[b] = stage.tile([P, max(BLOCKS) * NODES], U32, align_bytes=64, name="codes")
            scales_of[b] = stage.tile([P, max(BLOCKS) * NODES], U8, align_bytes=64, name="scales")
            nc.vector.quantize_mx(
                out=codes_of[b][:, 0 : n * NODES].bitcast(FP8X4),
                scales=scales_of[b][:, 0 : n * NODES],
                in_=grouped_of[b][:, 0:n].rearrange("p j n t -> p (j n t)"),
            )

        def project_block(b):
            for i in range(BLOCKS[b]):
                cols = slice(NODES * i, NODES * (i + 1))
                z = psum_z.tile([P, FEATS], F32, tag="z")
                nc.tensor.matmul_mx(
                    out=z[:],
                    lhsT=codes_of[b][:, cols].bitcast(FP8X4),
                    lhsT_scale=scales_of[b][:, cols],
                    rhs=wq_words[:].bitcast(FP8X4),
                    rhs_scale=wq_plane[:],
                    start=True,
                    stop=True,
                )
                z_of[STARTS[b] + i] = z

        def kind(j):
            return KINDS[j % len(KINDS)]

        def new_term(j):
            term = terms.tile([P, PACK, P], F32, name="term")
            terms_of[j].append(term)
            return term

        def weigh_rest(engine, j):
            engine.tensor_scalar(
                out=new_term(j)[:], in0=mid_of[j][:], scalar1=weight[:, j : j + 1], scalar2=1.0 - NEG_SLOPE,
                op0=ALU.mult, op1=ALU.mult,
            )

        def begin(j):
            terms_of[j] = []
            mid = mids.tile([P, PACK, P], F32, name="mid")
            mid_of[j] = mid
            z = by_word(z_of[j])
            if kind(j) == "two":
                nc.vector.tensor_tensor(out=mid[:], in0=z, in1=bq_neg[:], op=ALU.max)
                nc.scalar.activation(out=new_term(j)[:], in_=z, func=ACT.Copy, scale=weight_slope[:, j : j + 1])
                if j != NGBRS - 1:
                    weigh_rest(nc.gpsimd, j)
            elif j != LAST:
                nc.vector.scalar_tensor_tensor(
                    out=mid[:], in0=z, scalar=NEG_SLOPE, in1=bq_low[:], op0=ALU.mult, op1=ALU.add
                )

        def finish(j):
            if kind(j) == "two" or j == LAST:
                return
            mid = mid_of[j]
            nc.vector.tensor_tensor(out=mid[:], in0=by_word(z_of[j]), in1=mid[:], op=ALU.max)
            if kind(j) == "oneS" or j >= STARTS[-1]:
                nc.scalar.activation(out=new_term(j)[:], in_=mid[:], func=ACT.Copy, scale=weight[:, j : j + 1])
            else:
                nc.gpsimd.tensor_scalar(
                    out=new_term(j)[:], in0=mid[:], scalar1=weight[:, j : j + 1], scalar2=1.0,
                    op0=ALU.mult, op1=ALU.mult,
                )

        def finish_last(j):
            z, mid, term = by_word(z_of[j]), mid_of[j], new_term(j)
            halves = [slice(0, PACK // 2), slice(PACK // 2, PACK)]
            for t in halves:
                nc.vector.scalar_tensor_tensor(
                    out=mid[:, t], in0=z[:, t], scalar=NEG_SLOPE, in1=bq_low[:, t], op0=ALU.mult, op1=ALU.add
                )
            weigh_rest(nc.vector, NGBRS - 1)
            for t in halves:
                nc.vector.tensor_tensor(out=mid[:, t], in0=z[:, t], in1=mid[:, t], op=ALU.max)
            for t in halves:
                nc.vector.tensor_scalar_mul(out=term[:, t], in0=mid[:, t], scalar1=weight[:, j : j + 1])

        def elementwise_block(b):
            first, n = STARTS[b], BLOCKS[b]
            for i in range(n + 1):
                if i < n:
                    begin(first + i)
                if i == 0:
                    if b + 1 < N_BLOCKS:
                        quantise_block(b + 1)
                    if b == 2:
                        quantise_node()
                for q, at in enumerate([0,0]):
                    if i == min(at, n) and b + 2 < N_BLOCKS and PAIR * q < BLOCKS[b + 2]:
                        collect_words(b + 2, PAIR * q)
                if i > 0:
                    finish(first + i - 1)

        n_sums = 1 + sum(2 if kind(j) == "two" else 1 for j in range(NGBRS))
        summed = []

        def sum_terms(js):
            for j in js:
                for term in terms_of[j]:
                    summed.append(term)
                    for t in range(PACK):
                        nc.tensor.matmul(
                            out=acc[:, t, :], lhsT=term[:, t, :], rhs=ident_f32[:], is_transpose=True,
                            start=(len(summed) == 1 and t == 0), stop=(len(summed) == n_sums and t == PACK - 1),
                        )

        node_grouped = consts.tile([P, NODES, PACK], BF16, align_bytes=64)

        def transpose_node():
            node_t = psum_z.tile([P, 2, NODES], F32, tag="z")
            for u in range(2):
                transpose_words(node_t[:, u, :], node_bf[:], u)
            nc.scalar.copy(out=node_grouped[:].bitcast(F32), in_=node_t[:].rearrange("p u n -> p n u"))

        def quantise_node():
            nc.vector.quantize_mx(
                out=concat_codes[:, 0, :].bitcast(FP8X4),
                scales=concat_scales[:, 0, :],
                in_=node_grouped[:].rearrange("p n t -> p (n t)"),
            )

        for i in range(2):
            idle = psum_z.tile([P, FEATS], F32, tag="z")
            nc.tensor.matmul(out=idle[:], lhsT=ones_bf16[:], rhs=warm_row[:], start=True, stop=True)
        transpose_block(0)
        bq_all = psum_z.tile([P, FEATS], F32, tag="z")
        nc.tensor.matmul(out=bq_all[:], lhsT=ones_bf16[:], rhs=bq_row[:], start=True, stop=True)
        for i in range(BLOCKS[0]):
            collect_words(0, i)
        bq_low = consts.tile([P, PACK, P], F32)
        nc.scalar.mul(out=bq_low[:], in_=by_word(bq_all), mul=NEG_SLOPE - 1.0)
        transpose_block(1)
        for i in range(0, BLOCKS[1], PAIR):
            collect_words(1, i)
        bq_neg = consts.tile([P, PACK, P], F32)
        nc.scalar.mul(out=bq_neg[:], in_=by_word(bq_all), mul=-1.0)
        quantise_block(0)
        bias_term = consts.tile([P, PACK, P], F32)
        nc.gpsimd.tensor_scalar(
            out=bias_term[:], in0=bq_neg[:], scalar1=weight_sum[:, 0:1], scalar2=-1.0, op0=ALU.mult, op1=ALU.mult
        )
        terms_of["bias"] = [bias_term]
        halves = [slice(0, FEATS // 2), slice(FEATS // 2, FEATS)]
        z2_of = []

        def second_pass(i, cols, part):
            nc.tensor.matmul_mx(
                out=z2_of[i][:],
                lhsT=concat_codes[:, part, :].bitcast(FP8X4),
                lhsT_scale=concat_scales[:, part, :],
                rhs=ww_words[:, part, cols].bitcast(FP8X4),
                rhs_scale=ww_planes[:, part, cols],
                start=(part == 0),
                stop=(part == 1),
            )

        for step in range(N_BLOCKS + 1):
            if step < N_BLOCKS:
                project_block(step)
            if step == N_BLOCKS - 2:
                for i, cols in enumerate(halves):
                    z2 = psum_in.tile([P, FEATS // 2], F32, tag="in")
                    z2_of.append(z2)
                    second_pass(i, cols, 0)
            if step == 1:
                transpose_node()
            if step + 2 < N_BLOCKS:
                transpose_block(step + 2)
            if step == 2:
                sum_terms(["bias"])
            if step >= 2:
                block = range(STARTS[step - 1] if step > 2 else 0, STARTS[step - 1] + BLOCKS[step - 1])
                sum_terms(sorted([j for j in block if j != LAST], key=lambda j: (j >= STARTS[-1] and kind(j) != "two")))
            if step == N_BLOCKS:
                sum_terms([LAST])
            if step < N_BLOCKS:
                elementwise_block(step)
            if step == N_BLOCKS - 1:
                finish_last(LAST)

        agg_grouped = consts.tile([P, NODES, PACK], BF16, align_bytes=64)
        node_halves = [slice(0, NODES // 2), slice(NODES // 2, NODES)]
        for rows in node_halves:
            nc.vector.tensor_copy(out=agg_grouped[:, rows, :], in_=acc[:, :, rows].rearrange("p t n -> p n t"))
        for rows in node_halves:
            nc.vector.quantize_mx(
                out=concat_codes[:, 1, rows].bitcast(FP8X4),
                scales=concat_scales[:, 1, rows],
                in_=agg_grouped[:, rows, :].rearrange("p n t -> p (n t)"),
            )
        for i, cols in enumerate(halves):
            second_pass(i, cols, 1)
        biased2 = consts.tile([P, FEATS], F32)
        h2 = consts.tile([P, FEATS], F32)
        squares = consts.tile([P, FEATS], F32)
        sum_sq = [consts.tile([P, 1], F32, name="sum_sq%d" % i) for i in range(2)]
        for i, cols in enumerate(halves):
            nc.vector.tensor_tensor(out=biased2[:, cols], in0=z2_of[i][:], in1=bw_all[:, cols], op=ALU.add)
        for i, cols in enumerate(halves):
            nc.vector.scalar_tensor_tensor(
                out=h2[:, cols], in0=biased2[:, cols], scalar=NEG_SLOPE, in1=biased2[:, cols],
                op0=ALU.mult, op1=ALU.max,
            )
            nc.scalar.activation(out=squares[:, cols], in_=h2[:, cols], func=ACT.Square, accum_out=sum_sq[i][:])
        sum_floor = consts.tile([P, 1], F32)
        nc.vector.tensor_scalar_max(out=sum_floor[:], in0=sum_sq[0][:], scalar1=TINY)
        norm_inv = consts.tile([P, 1], F32)
        nc.scalar.activation(
            out=norm_inv[:], in_=sum_sq[1][:], func=ACT.Abs_reciprocal_sqrt, bias=sum_floor[:, 0:1], scale=1.0
        )
        result = consts.tile([P, FEATS], F32)
        for cols, queue in zip(halves, [nc.sync, nc.scalar]):
            nc.vector.tensor_scalar_mul(out=result[:, cols], in0=h2[:, cols], scalar1=norm_inv[:, 0:1])
            queue.dma_start(out=out[:, cols], in_=result[:, cols])
